import numpy as np
import ml_dtypes


def mxq(x, axis, fmt="e4m3"):
    dtype, down = {"e4m3": (ml_dtypes.float8_e4m3fn, 7), "e5m2": (ml_dtypes.float8_e5m2, 14)}[fmt]
    v = np.moveaxis(np.asarray(x, np.float32).astype(ml_dtypes.bfloat16).astype(np.float64), axis, -1)
    blocks = v.reshape(v.shape[:-1] + (-1, 32))
    amax = np.abs(blocks).max(-1, keepdims=True)
    byte = np.maximum(np.where(amax > 0, np.frexp(amax)[1] - 1 + 127, 0) - down, 1)
    scale = np.exp2(byte - 127.0)
    codes = (blocks / scale).astype(np.float32).astype(dtype).astype(np.float64)
    return np.moveaxis((codes * scale).reshape(v.shape), -1, axis)


WIDE = False


def mx_kscale(k):
    if not WIDE:
        return np.ones(k)
    levels = np.array([10, -10, 5, -5, 0])
    a = np.random.permutation(np.resize(levels, k // 512 * 4)).reshape(k // 512, 4)
    idx = np.arange(k)
    return np.exp2(a[idx // 512, idx % 128 // 32])


BF16 = ml_dtypes.bfloat16


def bf(x):
    return np.asarray(x, np.float32).astype(BF16)


def f64(x):
    return np.asarray(x).astype(np.float64)


E2M1 = np.array([0.0, 0.5, 1.0, 1.5, 2.0, 3.0, 4.0, 6.0, -0.0, -0.5, -1.0, -1.5, -2.0, -3.0, -4.0, -6.0])


def pack_weight(w, fmt):
    k, n = w.shape
    w = f64(bf(w)).reshape(k // 32, 32, n)
    amax = np.abs(w).max(1)
    if fmt == "e4m3":
        byte = np.frexp(amax)[1] - 1 + 127 - 7
    else:
        mant, ex = np.frexp(amax / 6.0)
        byte = np.where(mant > 0.5, ex, ex - 1) + 127
    byte = np.clip(np.where(amax > 0, byte, 1), 1, 254)
    scaled = (w * np.exp2(127.0 - byte)[:, None, :]).reshape(k, n).astype(np.float32)
    by_word = np.ascontiguousarray(scaled.reshape(k // 512, 128, 4, n).transpose(0, 1, 3, 2))
    if fmt == "e4m3":
        words = by_word.astype(ml_dtypes.float8_e4m3fn).view(np.uint8)
    else:
        c = by_word.astype(ml_dtypes.float4_e2m1fn).view(np.uint8) & 0xF
        words = c[..., 0::2] | (c[..., 1::2] << 4)
    return np.ascontiguousarray(words), np.ascontiguousarray(byte.astype(np.uint8).reshape(k // 512, 16, n))


def unpack_weight(words, scales, fmt):
    g, p, n, _ = words.shape
    if fmt == "e4m3":
        vals = np.ascontiguousarray(words).view(ml_dtypes.float8_e4m3fn).astype(np.float64)
    else:
        nib = np.empty((g, p, n, 4), np.uint8)
        nib[..., 0::2] = words & 0xF
        nib[..., 1::2] = words >> 4
        vals = E2M1[nib]
    vals = vals * np.repeat(np.exp2(scales.astype(np.float64) - 127.0), 8, axis=1)[..., None]
    return vals.transpose(0, 1, 3, 2).reshape(g * 512, n)

def pack4(w):
    words, scales = pack_weight(w, "e2m1")
    return words.reshape(words.shape[0], 128, -1), scales


def unpack4(words, scales):
    return unpack_weight(words.reshape(words.shape[0], 128, -1, 2), scales, "e2m1")


B, S, H = 8, 129, 1024
N = B * (S - 1)
G = 0.75


def setup_inputs():
    s = mx_kscale(H)
    x = bf(np.random.standard_normal((B, S, H)) * s)
    k1 = bf(np.random.standard_normal((N, H)) * G * s)
    k2 = bf(np.random.standard_normal((N, H)) * G * np.sqrt(1.0 + 0.25 * G * G) * s)
    coefficients = np.random.standard_normal((H, H)) * G / np.sqrt(H) * s[:, None] / s[None, :]
    words, scales = pack4(np.ascontiguousarray(coefficients.T))
    return {"x": x,
            "k1": k1,
            "k2": k2,
            "coefficients_words": words,
            "coefficients_scales": scales}


def reference(x, k1, k2, coefficients_words, coefficients_scales):
    x, k1, k2 = f64(x), f64(k1), f64(k2)
    y = x[:, :-1, :].reshape(-1, H)
    ct = unpack4(coefficients_words, coefficients_scales)
    k3 = mxq(y + 0.5 * k2, 1, "e4m3") @ ct
    k4 = mxq(y + k3, 1, "e4m3") @ ct
    y1 = y + (k1 + 2.0 * k2 + 2.0 * k3 + k4) / 6.0
    return y1.reshape(B, S - 1, H) - x[:, 1:, :]

@@ -1,0 +1,172 @@
+from contextlib import ExitStack
+
+import concourse.masks as masks
+import concourse.mybir as mybir
+
+F32 = mybir.dt.float32
+BF16 = mybir.dt.bfloat16
+I32 = mybir.dt.int32
+U32 = mybir.dt.uint32
+U8 = mybir.dt.uint8
+FP8X4 = mybir.dt.float8_e4m3fn_x4
+FP4X4 = mybir.dt.float4_e2m1fn_x4
+MULT = mybir.AluOpType.mult
+ADD = mybir.AluOpType.add
+SUBTRACT = mybir.AluOpType.subtract
+
+P = 128
+B = 8
+H = 1024
+K_PASS = 512
+PASSES = H // K_PASS
+N_TILE = 512
+HALVES = H // N_TILE
+
+FLOPS = 2 * 2 * (B * P) * H * H
+
+
+def tile_sindylossmixin_pa_kernel(
+    tc, x, k1, k2, coefficients_words, coefficients_scales, out
+):
+    nc = tc.nc
+    with ExitStack() as ctx:
+        ctx.enter_context(tc.manual_schedule())
+        const = ctx.enter_context(tc.tile_pool(name="const", bufs=1))
+        inputs = ctx.enter_context(tc.tile_pool(name="inputs", bufs=1))
+        states = ctx.enter_context(tc.tile_pool(name="states", bufs=2))
+        sums = ctx.enter_context(tc.tile_pool(name="sums", bufs=4))
+        operands = ctx.enter_context(tc.tile_pool(name="operands", bufs=4))
+        psum_turned = ctx.enter_context(tc.psum_pool(name="psum_turned", bufs=2))
+        psum_product = ctx.enter_context(tc.psum_pool(name="psum_product", bufs=6))
+
+        identity = const.tile([P, P], F32)
+        masks.make_identity(nc, identity[:])
+
+        w_words = const.tile([P, PASSES, 2 * H], U8, align_bytes=64)
+        w_scales = const.tile([P, PASSES, H], U8, align_bytes=64)
+        w_scale_words = w_scales[:].bitcast(I32)
+        nc.vector.memset(w_scale_words, 0)
+
+        y_all = inputs.tile([P, B, H], BF16)
+        next_all = inputs.tile([P, B, H], BF16)
+        k1_all = inputs.tile([P, B, H], BF16)
+        k2_all = inputs.tile([P, B, H], BF16)
+
+        for b in range(B):
+            rows = slice(b * P, (b + 1) * P)
+            nc.sync.dma_start(out=y_all[:, b, :], in_=x[b, 0:P, :])
+            nc.sync.dma_start(out=k2_all[:, b, :], in_=k2[rows, :])
+            if b == 0:
+                for r in range(4):
+                    nc.sync.dma_start(
+                        out=w_scale_words[r:P:32, :, :],
+                        in_=coefficients_scales[:, r:16:4, :]
+                        .bitcast(I32)
+                        .rearrange("g q c -> q g c"),
+                    )
+                nc.sync.dma_start(
+                    out=w_words[:].bitcast(I32),
+                    in_=coefficients_words.bitcast(I32).rearrange("g p c -> p g c"),
+                )
+            nc.sync.dma_start(out=k1_all[:, b, :], in_=k1[rows, :])
+            nc.sync.dma_start(out=next_all[:, b, :], in_=x[b, 1 : P + 1, :])
+
+        def sort_and_turn(state):
+            sorted_bf = operands.tile([P, H], BF16)
+            for g in range(PASSES):
+                cols = slice(g * K_PASS, (g + 1) * K_PASS)
+                nc.scalar.copy(
+                    out=sorted_bf[:, cols].rearrange("m (u p e) -> m p u e", u=2, e=2),
+                    in_=state[:, cols].rearrange("m (p u e) -> m p u e", u=2, e=2),
+                )
+            words = sorted_bf[:].bitcast(F32)
+            turned = psum_turned.tile([P, 2 * PASSES, P], F32)
+            for c in range(2 * PASSES):
+                nc.tensor.transpose(turned[:, c, :], words[:, c * P : (c + 1) * P], identity[:])
+            return turned
+
+        def regroup(turned):
+            grouped = operands.tile([P, H], BF16, align_bytes=64)
+            nc.scalar.copy(
+                out=grouped[:].bitcast(F32).rearrange("p (g m u) -> p g m u", g=PASSES, u=2),
+                in_=turned[:].rearrange("p (g u) m -> p g m u", u=2),
+            )
+            return grouped
+
+        def quantise(grouped):
+            codes = operands.tile([P, PASSES * P], U32, align_bytes=64)
+            scales = operands.tile([P, PASSES * P], U8, align_bytes=64)
+            nc.vector.quantize_mx(out=codes[:].bitcast(FP8X4), scales=scales[:], in_=grouped[:])
+            return codes, scales
+
+        def times_w(codes, scales):
+            halves = []
+            for h in range(HALVES):
+                product = psum_product.tile([P, N_TILE], F32)
+                for g in range(PASSES):
+                    rows = slice(g * P, (g + 1) * P)
+                    nc.tensor.matmul_mx(
+                        out=product[:],
+                        lhsT=codes[:, rows].bitcast(FP8X4),
+                        lhsT_scale=scales[:, rows],
+                        rhs=w_words[:, g, 2 * h * N_TILE : 2 * (h + 1) * N_TILE].bitcast(FP4X4),
+                        rhs_scale=w_scales[:, g, h * N_TILE : (h + 1) * N_TILE],
+                        start=(g == 0),
+                        stop=(g == PASSES - 1),
+                    )
+                halves.append(product)
+            return halves
+
+        state1, state2, total, turned1, turned2, k3, k4 = {}, {}, {}, {}, {}, {}, {}
+
+        for i in range(-1, B + 1):
+            ahead, here, behind = i + 1, i, i - 1
+            if ahead < B:
+                state1[ahead] = states.tile([P, H], F32, name="state1")
+                nc.vector.scalar_tensor_tensor(
+                    out=state1[ahead][:], in0=k2_all[:, ahead, :], scalar=0.5,
+                    in1=y_all[:, ahead, :], op0=MULT, op1=ADD,
+                )
+                turned1[ahead] = sort_and_turn(state1[ahead])
+            if 0 <= here < B:
+                state2[here] = states.tile([P, H], F32, name="state2")
+                for h in range(HALVES):
+                    cols = slice(h * N_TILE, (h + 1) * N_TILE)
+                    nc.vector.tensor_tensor(
+                        out=state2[here][:, cols], in0=k3[here][h][:], in1=y_all[:, here, cols], op=ADD
+                    )
+                turned2[here] = sort_and_turn(state2[here])
+            if ahead < B:
+                grouped1 = regroup(turned1[ahead])
+            if 0 <= here < B:
+                grouped2 = regroup(turned2[here])
+            if ahead < B:
+                total[ahead] = sums.tile([P, H], F32, name="total")
+                nc.vector.scalar_tensor_tensor(
+                    out=total[ahead][:], in0=k1_all[:, ahead, :], scalar=1.0 / 6.0,
+                    in1=next_all[:, ahead, :], op0=MULT, op1=SUBTRACT,
+                )
+            if 0 <= here < B:
+                nc.vector.scalar_tensor_tensor(
+                    out=total[here][:], in0=state2[here][:], scalar=1.0 / 3.0,
+                    in1=total[here][:], op0=MULT, op1=ADD,
+                )
+            if ahead < B:
+                codes1, scales1 = quantise(grouped1)
+                k3[ahead] = times_w(codes1, scales1)
+            if 0 <= here < B:
+                codes2, scales2 = quantise(grouped2)
+                k4[here] = times_w(codes2, scales2)
+            if ahead < B:
+                nc.vector.scalar_tensor_tensor(
+                    out=total[ahead][:], in0=state1[ahead][:], scalar=2.0 / 3.0,
+                    in1=total[ahead][:], op0=MULT, op1=ADD,
+                )
+            if behind >= 0:
+                for h in range(HALVES):
+                    cols = slice(h * N_TILE, (h + 1) * N_TILE)
+                    nc.vector.scalar_tensor_tensor(
+                        out=total[behind][:, cols], in0=k4[behind][h][:], scalar=1.0 / 6.0,
+                        in1=total[behind][:, cols], op0=MULT, op1=ADD,
+                    )
+                    nc.sync.dma_start(out=out[behind, :, cols], in_=total[behind][:, cols])

@@ -13,6 +13,7 @@ FP4X4 = mybir.dt.float4_e2m1fn_x4
 MULT = mybir.AluOpType.mult
 ADD = mybir.AluOpType.add
 SUBTRACT = mybir.AluOpType.subtract
+COPY = mybir.ActivationFunctionType.Copy
 
 P = 128
 B = 8
@@ -24,6 +25,9 @@ HALVES = H // N_TILE
 
 FLOPS = 2 * 2 * (B * P) * H * H
 
+FIRST_ON_TENSOR = 2
+assert (B - FIRST_ON_TENSOR) * 2 * HALVES * 2 * P * P * N_TILE <= FLOPS // 10
+
 
 def tile_sindylossmixin_pa_kernel(
     tc, x, k1, k2, coefficients_words, coefficients_scales, out
@@ -34,13 +38,17 @@ def tile_sindylossmixin_pa_kernel(
         const = ctx.enter_context(tc.tile_pool(name="const", bufs=1))
         inputs = ctx.enter_context(tc.tile_pool(name="inputs", bufs=1))
         states = ctx.enter_context(tc.tile_pool(name="states", bufs=2))
-        sums = ctx.enter_context(tc.tile_pool(name="sums", bufs=4))
+        sums = ctx.enter_context(tc.tile_pool(name="sums", bufs=6))
         operands = ctx.enter_context(tc.tile_pool(name="operands", bufs=4))
         psum_turned = ctx.enter_context(tc.psum_pool(name="psum_turned", bufs=2))
-        psum_product = ctx.enter_context(tc.psum_pool(name="psum_product", bufs=6))
+        psum_banks = ctx.enter_context(tc.psum_pool(name="psum_banks", bufs=HALVES))
 
         identity = const.tile([P, P], F32)
         masks.make_identity(nc, identity[:])
+        four_eye = const.tile([P, P], BF16)
+        two_eye = const.tile([P, P], BF16)
+        nc.vector.tensor_scalar_mul(out=four_eye[:], in0=identity[:], scalar1=4.0)
+        nc.vector.tensor_scalar_mul(out=two_eye[:], in0=identity[:], scalar1=2.0)
 
         w_words = const.tile([P, PASSES, 2 * H], U8, align_bytes=64)
         w_scales = const.tile([P, PASSES, H], U8, align_bytes=64)
@@ -52,32 +60,51 @@ def tile_sindylossmixin_pa_kernel(
         k1_all = inputs.tile([P, B, H], BF16)
         k2_all = inputs.tile([P, B, H], BF16)
 
-        for b in range(B):
-            rows = slice(b * P, (b + 1) * P)
-            nc.sync.dma_start(out=y_all[:, b, :], in_=x[b, 0:P, :])
-            nc.sync.dma_start(out=k2_all[:, b, :], in_=k2[rows, :])
-            if b == 0:
-                for r in range(4):
-                    nc.sync.dma_start(
-                        out=w_scale_words[r:P:32, :, :],
-                        in_=coefficients_scales[:, r:16:4, :]
-                        .bitcast(I32)
-                        .rearrange("g q c -> q g c"),
-                    )
-                nc.sync.dma_start(
-                    out=w_words[:].bitcast(I32),
-                    in_=coefficients_words.bitcast(I32).rearrange("g p c -> p g c"),
-                )
-            nc.sync.dma_start(out=k1_all[:, b, :], in_=k1[rows, :])
-            nc.sync.dma_start(out=next_all[:, b, :], in_=x[b, 1 : P + 1, :])
+        def exists(b):
+            return 0 <= b < B
 
-        def sort_and_turn(state):
+        def half(h):
+            return slice(h * N_TILE, (h + 1) * N_TILE)
+
+        def load_w():
+            for r in range(4):
+                nc.sync.dma_start(
+                    out=w_scale_words[r:P:32, :, :],
+                    in_=coefficients_scales[:, r:16:4, :].bitcast(I32).rearrange("g q c -> q g c"),
+                )
+            nc.sync.dma_start(
+                out=w_words[:].bitcast(I32),
+                in_=coefficients_words.bitcast(I32).rearrange("g p c -> p g c"),
+            )
+
+        def state1_on_vector(b):
+            state = states.tile([P, H], F32, name="state1")
+            nc.vector.scalar_tensor_tensor(
+                out=state[:], in0=k2_all[:, b, :], scalar=0.5, in1=y_all[:, b, :], op0=MULT, op1=ADD
+            )
+            return [state[:, half(h)] for h in range(HALVES)]
+
+        def state1_on_tensor(b):
+            halves = []
+            for h in range(HALVES):
+                fourfold = psum_banks.tile([P, N_TILE], F32, name="fourfold")
+                nc.tensor.matmul(
+                    out=fourfold[:], lhsT=four_eye[:], rhs=y_all[:, b, half(h)], start=True, stop=False
+                )
+                nc.tensor.matmul(
+                    out=fourfold[:], lhsT=two_eye[:], rhs=k2_all[:, b, half(h)], start=False, stop=True
+                )
+                halves.append(fourfold[:])
+            return halves
+
+        def sort_and_turn(halves, unit):
             sorted_bf = operands.tile([P, H], BF16)
             for g in range(PASSES):
-                cols = slice(g * K_PASS, (g + 1) * K_PASS)
-                nc.scalar.copy(
-                    out=sorted_bf[:, cols].rearrange("m (u p e) -> m p u e", u=2, e=2),
-                    in_=state[:, cols].rearrange("m (p u e) -> m p u e", u=2, e=2),
+                nc.scalar.activation(
+                    out=sorted_bf[:, half(g)].rearrange("m (u p e) -> m p u e", u=2, e=2),
+                    in_=halves[g].rearrange("m (p u e) -> m p u e", u=2, e=2),
+                    func=COPY,
+                    scale=unit,
                 )
             words = sorted_bf[:].bitcast(F32)
             turned = psum_turned.tile([P, 2 * PASSES, P], F32)
@@ -93,16 +120,13 @@ def tile_sindylossmixin_pa_kernel(
             )
             return grouped
 
-        def quantise(grouped):
+        def quantise_and_multiply(grouped, name):
             codes = operands.tile([P, PASSES * P], U32, align_bytes=64)
             scales = operands.tile([P, PASSES * P], U8, align_bytes=64)
             nc.vector.quantize_mx(out=codes[:].bitcast(FP8X4), scales=scales[:], in_=grouped[:])
-            return codes, scales
-
-        def times_w(codes, scales):
             halves = []
             for h in range(HALVES):
-                product = psum_product.tile([P, N_TILE], F32)
+                product = psum_banks.tile([P, N_TILE], F32, name=name)
                 for g in range(PASSES):
                     rows = slice(g * P, (g + 1) * P)
                     nc.tensor.matmul_mx(
@@ -110,63 +134,64 @@ def tile_sindylossmixin_pa_kernel(
                         lhsT=codes[:, rows].bitcast(FP8X4),
                         lhsT_scale=scales[:, rows],
                         rhs=w_words[:, g, 2 * h * N_TILE : 2 * (h + 1) * N_TILE].bitcast(FP4X4),
-                        rhs_scale=w_scales[:, g, h * N_TILE : (h + 1) * N_TILE],
+                        rhs_scale=w_scales[:, g, half(h)],
                         start=(g == 0),
                         stop=(g == PASSES - 1),
                     )
-                halves.append(product)
+                halves.append(product[:])
             return halves
 
-        state1, state2, total, turned1, turned2, k3, k4 = {}, {}, {}, {}, {}, {}, {}
+        def add_scaled(total, term, factor):
+            nc.vector.scalar_tensor_tensor(
+                out=total, in0=term, scalar=factor, in1=total, op0=MULT, op1=ADD
+            )
 
-        for i in range(-1, B + 1):
-            ahead, here, behind = i + 1, i, i - 1
-            if ahead < B:
-                state1[ahead] = states.tile([P, H], F32, name="state1")
-                nc.vector.scalar_tensor_tensor(
-                    out=state1[ahead][:], in0=k2_all[:, ahead, :], scalar=0.5,
-                    in1=y_all[:, ahead, :], op0=MULT, op1=ADD,
-                )
-                turned1[ahead] = sort_and_turn(state1[ahead])
-            if 0 <= here < B:
-                state2[here] = states.tile([P, H], F32, name="state2")
+        for i in range(-2, B):
+            if exists(i + 2):
+                nc.sync.dma_start(out=y_all[:, i + 2, :], in_=x[i + 2, 0:P, :])
+                nc.sync.dma_start(out=k2_all[:, i + 2, :], in_=k2[(i + 2) * P : (i + 3) * P, :])
+                nc.sync.dma_start(out=next_all[:, i + 2, :], in_=x[i + 2, 1 : P + 1, :])
+            if exists(i):
+                nc.sync.dma_start(out=k1_all[:, i, :], in_=k1[i * P : (i + 1) * P, :])
+            if i == -1:
+                load_w()
+
+        state1, unit1, state2, total, grouped1, grouped2, k3, k4 = {}, {}, {}, {}, {}, {}, {}, {}
+        for i in range(-2, B + 1):
+            if exists(i + 2) and i + 2 < FIRST_ON_TENSOR:
+                state1[i + 2], unit1[i + 2] = state1_on_vector(i + 2), 1.0
+            if exists(i):
+                state2[i] = states.tile([P, H], F32, name="state2")
                 for h in range(HALVES):
-                    cols = slice(h * N_TILE, (h + 1) * N_TILE)
                     nc.vector.tensor_tensor(
-                        out=state2[here][:, cols], in0=k3[here][h][:], in1=y_all[:, here, cols], op=ADD
+                        out=state2[i][:, half(h)], in0=k3[i][h], in1=y_all[:, i, half(h)], op=ADD
                     )
-                turned2[here] = sort_and_turn(state2[here])
-            if ahead < B:
-                grouped1 = regroup(turned1[ahead])
-            if 0 <= here < B:
-                grouped2 = regroup(turned2[here])
-            if ahead < B:
-                total[ahead] = sums.tile([P, H], F32, name="total")
-                nc.vector.scalar_tensor_tensor(
-                    out=total[ahead][:], in0=k1_all[:, ahead, :], scalar=1.0 / 6.0,
-                    in1=next_all[:, ahead, :], op0=MULT, op1=SUBTRACT,
-                )
-            if 0 <= here < B:
-                nc.vector.scalar_tensor_tensor(
-                    out=total[here][:], in0=state2[here][:], scalar=1.0 / 3.0,
-                    in1=total[here][:], op0=MULT, op1=ADD,
-                )
-            if ahead < B:
-                codes1, scales1 = quantise(grouped1)
-                k3[ahead] = times_w(codes1, scales1)
-            if 0 <= here < B:
-                codes2, scales2 = quantise(grouped2)
-                k4[here] = times_w(codes2, scales2)
-            if ahead < B:
-                nc.vector.scalar_tensor_tensor(
-                    out=total[ahead][:], in0=state1[ahead][:], scalar=2.0 / 3.0,
-                    in1=total[ahead][:], op0=MULT, op1=ADD,
-                )
-            if behind >= 0:
+                turned2 = sort_and_turn([state2[i][:, half(h)] for h in range(HALVES)], 1.0)
+            if exists(i + 2):
+                turned1 = sort_and_turn(state1[i + 2], unit1[i + 2])
+            if exists(i):
+                grouped2[i] = regroup(turned2)
+            if exists(i + 2):
+                grouped1[i + 2] = regroup(turned1)
+            if exists(i + 1):
+                k3[i + 1] = quantise_and_multiply(grouped1[i + 1], "k3")
+            if exists(i + 3) and i + 3 >= FIRST_ON_TENSOR:
+                state1[i + 3], unit1[i + 3] = state1_on_tensor(i + 3), 0.25
+            if exists(i):
+                add_scaled(total[i][:], k1_all[:, i, :], 1.0 / 6.0)
+            if exists(i + 2):
+                total[i + 2] = sums.tile([P, H], F32, name="total")
                 for h in range(HALVES):
-                    cols = slice(h * N_TILE, (h + 1) * N_TILE)
                     nc.vector.scalar_tensor_tensor(
-                        out=total[behind][:, cols], in0=k4[behind][h][:], scalar=1.0 / 6.0,
-                        in1=total[behind][:, cols], op0=MULT, op1=ADD,
+                        out=total[i + 2][:, half(h)], in0=state1[i + 2][h],
+                        scalar=unit1[i + 2] * 2.0 / 3.0,
+                        in1=next_all[:, i + 2, half(h)], op0=MULT, op1=SUBTRACT,
                     )
-                    nc.sync.dma_start(out=out[behind, :, cols], in_=total[behind][:, cols])
+            if exists(i):
+                add_scaled(total[i][:], state2[i][:], 1.0 / 3.0)
+            if exists(i - 1):
+                for h in range(HALVES):
+                    add_scaled(total[i - 1][:, half(h)], k4[i - 1][h], 1.0 / 6.0)
+                    nc.sync.dma_start(out=out[i - 1, :, half(h)], in_=total[i - 1][:, half(h)])
+            if exists(i):
+                k4[i] = quantise_and_multiply(grouped2[i], "k4")

@@ -38,7 +38,7 @@ def tile_sindylossmixin_pa_kernel(
         const = ctx.enter_context(tc.tile_pool(name="const", bufs=1))
         inputs = ctx.enter_context(tc.tile_pool(name="inputs", bufs=1))
         states = ctx.enter_context(tc.tile_pool(name="states", bufs=2))
-        sums = ctx.enter_context(tc.tile_pool(name="sums", bufs=6))
+        sums = ctx.enter_context(tc.tile_pool(name="sums", bufs=7))
         operands = ctx.enter_context(tc.tile_pool(name="operands", bufs=4))
         psum_turned = ctx.enter_context(tc.psum_pool(name="psum_turned", bufs=2))
         psum_banks = ctx.enter_context(tc.psum_pool(name="psum_banks", bufs=HALVES))
@@ -146,20 +146,34 @@ def tile_sindylossmixin_pa_kernel(
                 out=total, in0=term, scalar=factor, in1=total, op0=MULT, op1=ADD
             )
 
-        for i in range(-2, B):
-            if exists(i + 2):
-                nc.sync.dma_start(out=y_all[:, i + 2, :], in_=x[i + 2, 0:P, :])
-                nc.sync.dma_start(out=k2_all[:, i + 2, :], in_=k2[(i + 2) * P : (i + 3) * P, :])
-                nc.sync.dma_start(out=next_all[:, i + 2, :], in_=x[i + 2, 1 : P + 1, :])
-            if exists(i):
-                nc.sync.dma_start(out=k1_all[:, i, :], in_=k1[i * P : (i + 1) * P, :])
-            if i == -1:
+        for b in range(B):
+            nc.sync.dma_start(out=y_all[:, b, :], in_=x[b, 0:P, :])
+            nc.sync.dma_start(out=k2_all[:, b, :], in_=k2[b * P : (b + 1) * P, :])
+            nc.sync.dma_start(out=k1_all[:, b, :], in_=k1[b * P : (b + 1) * P, :])
+            nc.sync.dma_start(out=next_all[:, b, :], in_=x[b, 1 : P + 1, :])
+            if b == 1:
                 load_w()
 
+        def base_on_vector(b):
+            base = sums.tile([P, H], F32, name="total")
+            nc.vector.scalar_tensor_tensor(
+                out=base[:], in0=k1_all[:, b, :], scalar=1.0 / 6.0, in1=next_all[:, b, :],
+                op0=MULT, op1=SUBTRACT,
+            )
+            return base
+
+        def base_beside_vector(b):
+            base = sums.tile([P, H], F32, name="total")
+            nc.scalar.activation(out=base[:], in_=k1_all[:, b, :], func=COPY, scale=1.0 / 6.0)
+            for h in range(HALVES):
+                nc.gpsimd.tensor_tensor(
+                    out=base[:, half(h)], in0=base[:, half(h)], in1=next_all[:, b, half(h)],
+                    op=SUBTRACT,
+                )
+            return base
+
         state1, unit1, state2, total, grouped1, grouped2, k3, k4 = {}, {}, {}, {}, {}, {}, {}, {}
-        for i in range(-2, B + 1):
-            if exists(i + 2) and i + 2 < FIRST_ON_TENSOR:
-                state1[i + 2], unit1[i + 2] = state1_on_vector(i + 2), 1.0
+        for i in range(-3, B + 1):
             if exists(i):
                 state2[i] = states.tile([P, H], F32, name="state2")
                 for h in range(HALVES):
@@ -177,21 +191,18 @@ def tile_sindylossmixin_pa_kernel(
                 k3[i + 1] = quantise_and_multiply(grouped1[i + 1], "k3")
             if exists(i + 3) and i + 3 >= FIRST_ON_TENSOR:
                 state1[i + 3], unit1[i + 3] = state1_on_tensor(i + 3), 0.25
-            if exists(i):
-                add_scaled(total[i][:], k1_all[:, i, :], 1.0 / 6.0)
-            if exists(i + 2):
-                total[i + 2] = sums.tile([P, H], F32, name="total")
-                for h in range(HALVES):
-                    nc.vector.scalar_tensor_tensor(
-                        out=total[i + 2][:, half(h)], in0=state1[i + 2][h],
-                        scalar=unit1[i + 2] * 2.0 / 3.0,
-                        in1=next_all[:, i + 2, half(h)], op0=MULT, op1=SUBTRACT,
-                    )
+                total[i + 3] = base_beside_vector(i + 3)
             if exists(i):
                 add_scaled(total[i][:], state2[i][:], 1.0 / 3.0)
+            if exists(i + 2):
+                for h in range(HALVES):
+                    add_scaled(total[i + 2][:, half(h)], state1[i + 2][h], unit1[i + 2] * 2.0 / 3.0)
             if exists(i - 1):
                 for h in range(HALVES):
                     add_scaled(total[i - 1][:, half(h)], k4[i - 1][h], 1.0 / 6.0)
                     nc.sync.dma_start(out=out[i - 1, :, half(h)], in_=total[i - 1][:, half(h)])
             if exists(i):
                 k4[i] = quantise_and_multiply(grouped2[i], "k4")
+            if exists(i + 3) and i + 3 < FIRST_ON_TENSOR:
+                state1[i + 3], unit1[i + 3] = state1_on_vector(i + 3), 1.0
+                total[i + 3] = base_on_vector(i + 3)

@@ -22,10 +22,12 @@ K_PASS = 512
 PASSES = H // K_PASS
 N_TILE = 512
 HALVES = H // N_TILE
+GPSIMD_PIECE = 256
 
 FLOPS = 2 * 2 * (B * P) * H * H
 
 FIRST_ON_TENSOR = 2
+FIRST_ON_GPSIMD = 4
 assert (B - FIRST_ON_TENSOR) * 2 * HALVES * 2 * P * P * N_TILE <= FLOPS // 10
 
 
@@ -38,7 +40,7 @@ def tile_sindylossmixin_pa_kernel(
         const = ctx.enter_context(tc.tile_pool(name="const", bufs=1))
         inputs = ctx.enter_context(tc.tile_pool(name="inputs", bufs=1))
         states = ctx.enter_context(tc.tile_pool(name="states", bufs=2))
-        sums = ctx.enter_context(tc.tile_pool(name="sums", bufs=7))
+        sums = ctx.enter_context(tc.tile_pool(name="sums", bufs=B))
         operands = ctx.enter_context(tc.tile_pool(name="operands", bufs=4))
         psum_turned = ctx.enter_context(tc.psum_pool(name="psum_turned", bufs=2))
         psum_banks = ctx.enter_context(tc.psum_pool(name="psum_banks", bufs=HALVES))
@@ -165,10 +167,10 @@ def tile_sindylossmixin_pa_kernel(
         def base_beside_vector(b):
             base = sums.tile([P, H], F32, name="total")
             nc.scalar.activation(out=base[:], in_=k1_all[:, b, :], func=COPY, scale=1.0 / 6.0)
-            for h in range(HALVES):
+            for c in range(0, H, GPSIMD_PIECE):
+                cols = slice(c, c + GPSIMD_PIECE)
                 nc.gpsimd.tensor_tensor(
-                    out=base[:, half(h)], in0=base[:, half(h)], in1=next_all[:, b, half(h)],
-                    op=SUBTRACT,
+                    out=base[:, cols], in0=base[:, cols], in1=next_all[:, b, cols], op=SUBTRACT
                 )
             return base
 
@@ -191,18 +193,20 @@ def tile_sindylossmixin_pa_kernel(
                 k3[i + 1] = quantise_and_multiply(grouped1[i + 1], "k3")
             if exists(i + 3) and i + 3 >= FIRST_ON_TENSOR:
                 state1[i + 3], unit1[i + 3] = state1_on_tensor(i + 3), 0.25
-                total[i + 3] = base_beside_vector(i + 3)
+            if exists(i + 4) and i + 4 >= FIRST_ON_GPSIMD:
+                total[i + 4] = base_beside_vector(i + 4)
             if exists(i):
                 add_scaled(total[i][:], state2[i][:], 1.0 / 3.0)
-            if exists(i + 2):
-                for h in range(HALVES):
-                    add_scaled(total[i + 2][:, half(h)], state1[i + 2][h], unit1[i + 2] * 2.0 / 3.0)
             if exists(i - 1):
                 for h in range(HALVES):
                     add_scaled(total[i - 1][:, half(h)], k4[i - 1][h], 1.0 / 6.0)
                     nc.sync.dma_start(out=out[i - 1, :, half(h)], in_=total[i - 1][:, half(h)])
+            if exists(i + 2):
+                for h in range(HALVES):
+                    add_scaled(total[i + 2][:, half(h)], state1[i + 2][h], unit1[i + 2] * 2.0 / 3.0)
             if exists(i):
                 k4[i] = quantise_and_multiply(grouped2[i], "k4")
             if exists(i + 3) and i + 3 < FIRST_ON_TENSOR:
                 state1[i + 3], unit1[i + 3] = state1_on_vector(i + 3), 1.0
+            if exists(i + 3) and i + 3 < FIRST_ON_GPSIMD:
                 total[i + 3] = base_on_vector(i + 3)

@@ -22,13 +22,18 @@ K_PASS = 512
 PASSES = H // K_PASS
 N_TILE = 512
 HALVES = H // N_TILE
-GPSIMD_PIECE = 256
+GPSIMD_PIECE = 512
 
 FLOPS = 2 * 2 * (B * P) * H * H
 
-FIRST_ON_TENSOR = 2
-FIRST_ON_GPSIMD = 4
-assert (B - FIRST_ON_TENSOR) * 2 * HALVES * 2 * P * P * N_TILE <= FLOPS // 10
+ON_TENSOR = (2, 4, 6)
+TENSOR_ROUND = {2: 0, 4: 2, 6: 4}
+FIRST = -2
+DOUBLED_ON_SCALAR = (2, 3, 4, 5, 6, 7)
+LEAD = 2
+MERGES = {-2: (0, 2), -1: (1, 1), 0: (1, 1), 1: (1, 0), 2: (1, 1), 3: (1, 0), 4: (1, 1), 5: (1, 0), 6: (1, 0), 7: (1, 1)}
+TWICE = (0, 1, 2, 3, 4, 5, 6, 7)
+assert len(ON_TENSOR) * 4 * HALVES * 2 * P * P * N_TILE <= FLOPS // 10
 
 
 def tile_sindylossmixin_pa_kernel(
@@ -39,23 +44,26 @@ def tile_sindylossmixin_pa_kernel(
         ctx.enter_context(tc.manual_schedule())
         const = ctx.enter_context(tc.tile_pool(name="const", bufs=1))
         inputs = ctx.enter_context(tc.tile_pool(name="inputs", bufs=1))
-        states = ctx.enter_context(tc.tile_pool(name="states", bufs=2))
         sums = ctx.enter_context(tc.tile_pool(name="sums", bufs=B))
         operands = ctx.enter_context(tc.tile_pool(name="operands", bufs=4))
         psum_turned = ctx.enter_context(tc.psum_pool(name="psum_turned", bufs=2))
-        psum_banks = ctx.enter_context(tc.psum_pool(name="psum_banks", bufs=HALVES))
+        psum_banks = ctx.enter_context(tc.psum_pool(name="psum_banks", bufs=6))
 
         identity = const.tile([P, P], F32)
         masks.make_identity(nc, identity[:])
-        four_eye = const.tile([P, P], BF16)
+        six_eye = const.tile([P, P], BF16)
+        minus_six_eye = const.tile([P, P], BF16)
+        one_eye = const.tile([P, P], BF16)
         two_eye = const.tile([P, P], BF16)
-        nc.vector.tensor_scalar_mul(out=four_eye[:], in0=identity[:], scalar1=4.0)
-        nc.vector.tensor_scalar_mul(out=two_eye[:], in0=identity[:], scalar1=2.0)
 
         w_words = const.tile([P, PASSES, 2 * H], U8, align_bytes=64)
         w_scales = const.tile([P, PASSES, H], U8, align_bytes=64)
         w_scale_words = w_scales[:].bitcast(I32)
         nc.vector.memset(w_scale_words, 0)
+        nc.vector.tensor_scalar_mul(out=six_eye[:], in0=identity[:], scalar1=6.0)
+        nc.vector.tensor_scalar_mul(out=minus_six_eye[:], in0=identity[:], scalar1=-6.0)
+        nc.vector.tensor_scalar_mul(out=one_eye[:], in0=identity[:], scalar1=1.0)
+        nc.vector.tensor_scalar_mul(out=two_eye[:], in0=identity[:], scalar1=2.0)
 
         y_all = inputs.tile([P, B, H], BF16)
         next_all = inputs.tile([P, B, H], BF16)
@@ -79,134 +87,180 @@ def tile_sindylossmixin_pa_kernel(
                 in_=coefficients_words.bitcast(I32).rearrange("g p c -> p g c"),
             )
 
-        def state1_on_vector(b):
-            state = states.tile([P, H], F32, name="state1")
-            nc.vector.scalar_tensor_tensor(
-                out=state[:], in0=k2_all[:, b, :], scalar=0.5, in1=y_all[:, b, :], op0=MULT, op1=ADD
-            )
-            return [state[:, half(h)] for h in range(HALVES)]
+        def load_state(b):
+            nc.sync.dma_start(out=y_all[:, b, :], in_=x[b, 0:P, :])
+            nc.sync.dma_start(out=k2_all[:, b, :], in_=k2[b * P : (b + 1) * P, :])
 
-        def state1_on_tensor(b):
-            halves = []
-            for h in range(HALVES):
-                fourfold = psum_banks.tile([P, N_TILE], F32, name="fourfold")
-                nc.tensor.matmul(
-                    out=fourfold[:], lhsT=four_eye[:], rhs=y_all[:, b, half(h)], start=True, stop=False
-                )
-                nc.tensor.matmul(
-                    out=fourfold[:], lhsT=two_eye[:], rhs=k2_all[:, b, half(h)], start=False, stop=True
-                )
-                halves.append(fourfold[:])
-            return halves
+        def load_rest(b):
+            nc.sync.dma_start(out=k1_all[:, b, :], in_=k1[b * P : (b + 1) * P, :])
+            nc.sync.dma_start(out=next_all[:, b, :], in_=x[b, 1 : P + 1, :])
 
-        def sort_and_turn(halves, unit):
-            sorted_bf = operands.tile([P, H], BF16)
+        def first_state(b):
+            pairs = operands.tile([P, H], BF16, name="pairs1")
+            if b in DOUBLED_ON_SCALAR:
+                twice = doubled_y[b]
+            else:
+                twice = operands.tile([P, H], BF16, name="twice")
+                nc.vector.tensor_scalar_mul(out=twice[:], in0=y_all[:, b, :], scalar1=2.0)
+            for u in range(2):
+                nc.vector.tensor_tensor(
+                    out=pairs[:, u * K_PASS : (u + 1) * K_PASS].rearrange("m (o q e) -> m o q e", o=1, e=2),
+                    in0=twice[:].rearrange("m (q u e) -> m u q e", u=2, e=2)[:, u : u + 1],
+                    in1=k2_all[:, b, :].rearrange("m (q u e) -> m u q e", u=2, e=2)[:, u : u + 1],
+                    op=ADD,
+                )
+            return pairs
+
+        def double_y(b):
+            twice = operands.tile([P, H], BF16, name="twice")
+            nc.scalar.activation(out=twice[:], in_=y_all[:, b, :], func=COPY, scale=2.0)
+            return twice
+
+        def second_state(b, doubled_k3):
+            pairs = operands.tile([P, H], BF16, name="pairs2")
             for g in range(PASSES):
-                nc.scalar.activation(
-                    out=sorted_bf[:, half(g)].rearrange("m (u p e) -> m p u e", u=2, e=2),
-                    in_=halves[g].rearrange("m (p u e) -> m p u e", u=2, e=2),
-                    func=COPY,
-                    scale=unit,
-                )
-            words = sorted_bf[:].bitcast(F32)
+                for u in range(2):
+                    first = u * K_PASS + g * 2 * P
+                    nc.vector.scalar_tensor_tensor(
+                        out=pairs[:, first : first + 2 * P].rearrange("m (o p e) -> m o p e", o=1, e=2),
+                        in0=doubled_k3[g].rearrange("m (p u e) -> m u p e", u=2, e=2)[:, u : u + 1],
+                        scalar=0.5,
+                        in1=y_all[:, b, half(g)].rearrange("m (p u e) -> m u p e", u=2, e=2)[:, u : u + 1],
+                        op0=MULT,
+                        op1=ADD,
+                    )
+            return pairs
+
+        def turn(pairs):
+            words = pairs[:].bitcast(F32)
             turned = psum_turned.tile([P, 2 * PASSES, P], F32)
-            for c in range(2 * PASSES):
-                nc.tensor.transpose(turned[:, c, :], words[:, c * P : (c + 1) * P], identity[:])
+            for g in range(PASSES):
+                for u in range(2):
+                    first = (u * PASSES + g) * P
+                    nc.tensor.transpose(turned[:, 2 * g + u, :], words[:, first : first + P], identity[:])
             return turned
 
-        def regroup(turned):
-            grouped = operands.tile([P, H], BF16, align_bytes=64)
+        def regroup(turned, name):
+            grouped = operands.tile([P, H], BF16, align_bytes=64, name=name)
             nc.scalar.copy(
                 out=grouped[:].bitcast(F32).rearrange("p (g m u) -> p g m u", g=PASSES, u=2),
                 in_=turned[:].rearrange("p (g u) m -> p g m u", u=2),
             )
             return grouped
 
-        def quantise_and_multiply(grouped, name):
-            codes = operands.tile([P, PASSES * P], U32, align_bytes=64)
-            scales = operands.tile([P, PASSES * P], U8, align_bytes=64)
+        def quantise(grouped, name):
+            codes = operands.tile([P, PASSES * P], U32, align_bytes=64, name="codes" + name)
+            scales = operands.tile([P, PASSES * P], U8, align_bytes=64, name="scales" + name)
             nc.vector.quantize_mx(out=codes[:].bitcast(FP8X4), scales=scales[:], in_=grouped[:])
-            halves = []
+            return codes, scales
+
+        def new_banks():
+            banks = []
             for h in range(HALVES):
-                product = psum_banks.tile([P, N_TILE], F32, name=name)
+                bank = psum_banks.tile([P, N_TILE], F32, name="bank")
+                banks.append(bank[:])
+            return banks
+
+        def multiply(banks, operand, opens, closes):
+            codes, scales = operand
+            for h in range(HALVES):
                 for g in range(PASSES):
                     rows = slice(g * P, (g + 1) * P)
                     nc.tensor.matmul_mx(
-                        out=product[:],
+                        out=banks[h],
                         lhsT=codes[:, rows].bitcast(FP8X4),
                         lhsT_scale=scales[:, rows],
                         rhs=w_words[:, g, 2 * h * N_TILE : 2 * (h + 1) * N_TILE].bitcast(FP4X4),
                         rhs_scale=w_scales[:, g, half(h)],
-                        start=(g == 0),
-                        stop=(g == PASSES - 1),
+                        start=(opens and g == 0),
+                        stop=(closes and g == PASSES - 1),
                     )
-                halves.append(product[:])
-            return halves
 
         def add_scaled(total, term, factor):
             nc.vector.scalar_tensor_tensor(
                 out=total, in0=term, scalar=factor, in1=total, op0=MULT, op1=ADD
             )
 
+        def base_on_tensor(b, h):
+            terms = ((six_eye, y_all), (minus_six_eye, next_all), (one_eye, k1_all), (two_eye, k2_all))
+            bank = psum_banks.tile([P, N_TILE], F32, name="bank")
+            for n, (eye, source) in enumerate(terms):
+                nc.tensor.matmul(
+                    out=bank[:], lhsT=eye[:], rhs=source[:, b, half(h)],
+                    start=(n == 0), stop=(n == len(terms) - 1),
+                )
+            return bank
+
+        def base_out_of_psum(base, bank, h):
+            nc.scalar.activation(out=base[:, half(h)], in_=bank[:], func=COPY, scale=1.0 / 6.0)
+
+        def base_on_vector(b, step, base):
+            if step == 0:
+                base = sums.tile([P, H], F32, name="total")
+                nc.vector.scalar_tensor_tensor(
+                    out=base[:], in0=k1_all[:, b, :], scalar=1.0 / 6.0, in1=next_all[:, b, :],
+                    op0=MULT, op1=SUBTRACT,
+                )
+            elif step == 1:
+                add_scaled(base[:], k2_all[:, b, :], 1.0 / 3.0)
+            else:
+                add_scaled(base[:], y_all[:, b, :], 1.0)
+            return base
+
         for b in range(B):
-            nc.sync.dma_start(out=y_all[:, b, :], in_=x[b, 0:P, :])
-            nc.sync.dma_start(out=k2_all[:, b, :], in_=k2[b * P : (b + 1) * P, :])
-            nc.sync.dma_start(out=k1_all[:, b, :], in_=k1[b * P : (b + 1) * P, :])
-            nc.sync.dma_start(out=next_all[:, b, :], in_=x[b, 1 : P + 1, :])
-            if b == 1:
+            load_state(b)
+            load_rest(b)
+            if b == 0:
                 load_w()
 
-        def base_on_vector(b):
-            base = sums.tile([P, H], F32, name="total")
-            nc.vector.scalar_tensor_tensor(
-                out=base[:], in0=k1_all[:, b, :], scalar=1.0 / 6.0, in1=next_all[:, b, :],
-                op0=MULT, op1=SUBTRACT,
-            )
-            return base
+        pairs1, grouped1, grouped2, operand1, operand2 = {}, {}, {}, {}, {}
+        doubled_k3, last, total, sixfold, doubled_y = {}, {}, {}, {}, {}
+        waiting = [(b, step) for b in range(B) if b not in ON_TENSOR for step in range(3)]
 
-        def base_beside_vector(b):
-            base = sums.tile([P, H], F32, name="total")
-            nc.scalar.activation(out=base[:], in_=k1_all[:, b, :], func=COPY, scale=1.0 / 6.0)
-            for c in range(0, H, GPSIMD_PIECE):
-                cols = slice(c, c + GPSIMD_PIECE)
-                nc.gpsimd.tensor_tensor(
-                    out=base[:, cols], in0=base[:, cols], in1=next_all[:, b, cols], op=SUBTRACT
-                )
-            return base
+        served = {"count": 0}
 
-        state1, unit1, state2, total, grouped1, grouped2, k3, k4 = {}, {}, {}, {}, {}, {}, {}, {}
-        for i in range(-3, B + 1):
+        def merges(count):
+            for n in range(count):
+                if served["count"] < len(waiting):
+                    b, step = waiting[served["count"]]
+                    served["count"] = served["count"] + 1
+                    total[b] = base_on_vector(b, step, total.get(b))
+
+        for i in range(FIRST, B + 1):
             if exists(i):
-                state2[i] = states.tile([P, H], F32, name="state2")
-                for h in range(HALVES):
-                    nc.vector.tensor_tensor(
-                        out=state2[i][:, half(h)], in0=k3[i][h], in1=y_all[:, i, half(h)], op=ADD
-                    )
-                turned2 = sort_and_turn([state2[i][:, half(h)] for h in range(HALVES)], 1.0)
-            if exists(i + 2):
-                turned1 = sort_and_turn(state1[i + 2], unit1[i + 2])
-            if exists(i):
-                grouped2[i] = regroup(turned2)
-            if exists(i + 2):
-                grouped1[i + 2] = regroup(turned1)
+                grouped2[i] = regroup(turn(second_state(i, doubled_k3[i])), "grouped2")
             if exists(i + 1):
-                k3[i + 1] = quantise_and_multiply(grouped1[i + 1], "k3")
-            if exists(i + 3) and i + 3 >= FIRST_ON_TENSOR:
-                state1[i + 3], unit1[i + 3] = state1_on_tensor(i + 3), 0.25
-            if exists(i + 4) and i + 4 >= FIRST_ON_GPSIMD:
-                total[i + 4] = base_beside_vector(i + 4)
+                operand1[i + 1] = quantise(grouped1[i + 1], "1")
+            if exists(i) and i in TWICE:
+                last[i] = new_banks()
+                multiply(last[i], operand1[i], True, False)
+            if exists(i + 1):
+                doubled_k3[i + 1] = new_banks()
+                multiply(doubled_k3[i + 1], operand1[i + 1], True, True)
+            merges(MERGES.get(i, (0, 0))[0])
             if exists(i):
-                add_scaled(total[i][:], state2[i][:], 1.0 / 3.0)
+                operand2[i] = quantise(grouped2[i], "2")
+                if i not in TWICE:
+                    last[i] = new_banks()
+                multiply(last[i], operand2[i], i not in TWICE, True)
             if exists(i - 1):
                 for h in range(HALVES):
-                    add_scaled(total[i - 1][:, half(h)], k4[i - 1][h], 1.0 / 6.0)
+                    add_scaled(total[i - 1][:, half(h)], last[i - 1][h], 1.0 / 6.0)
                     nc.sync.dma_start(out=out[i - 1, :, half(h)], in_=total[i - 1][:, half(h)])
-            if exists(i + 2):
+            if exists(i) and i not in TWICE:
                 for h in range(HALVES):
-                    add_scaled(total[i + 2][:, half(h)], state1[i + 2][h], unit1[i + 2] * 2.0 / 3.0)
-            if exists(i):
-                k4[i] = quantise_and_multiply(grouped2[i], "k4")
-            if exists(i + 3) and i + 3 < FIRST_ON_TENSOR:
-                state1[i + 3], unit1[i + 3] = state1_on_vector(i + 3), 1.0
-            if exists(i + 3) and i + 3 < FIRST_ON_GPSIMD:
-                total[i + 3] = base_on_vector(i + 3)
+                    add_scaled(total[i][:, half(h)], doubled_k3[i][h], 1.0 / 6.0)
+            if i + LEAD + 1 in DOUBLED_ON_SCALAR:
+                doubled_y[i + LEAD + 1] = double_y(i + LEAD + 1)
+            if exists(i + LEAD):
+                pairs1[i + LEAD] = first_state(i + LEAD)
+            if exists(i + 2):
+                grouped1[i + 2] = regroup(turn(pairs1[i + 2]), "grouped1")
+            merges(MERGES.get(i, (0, 0))[1])
+            for b in ON_TENSOR:
+                for h in range(HALVES):
+                    if TENSOR_ROUND[b] + h == i:
+                        sixfold[b, h] = base_on_tensor(b, h)
+                        if h == 0:
+                            total[b] = sums.tile([P, H], F32, name="total")
+                        base_out_of_psum(total[b], sixfold[b, h], h)

@@ -22,16 +22,17 @@ K_PASS = 512
 PASSES = H // K_PASS
 N_TILE = 512
 HALVES = H // N_TILE
-GPSIMD_PIECE = 512
+GPSIMD_PIECE = 256
 
 FLOPS = 2 * 2 * (B * P) * H * H
 
 ON_TENSOR = (2, 4, 6)
 TENSOR_ROUND = {2: 0, 4: 2, 6: 4}
 FIRST = -2
+DIFFERENCE_ON_GPSIMD = (1, 3, 5, 7)
 DOUBLED_ON_SCALAR = (2, 3, 4, 5, 6, 7)
 LEAD = 2
-MERGES = {-2: (0, 2), -1: (1, 1), 0: (1, 1), 1: (1, 0), 2: (1, 1), 3: (1, 0), 4: (1, 1), 5: (1, 0), 6: (1, 0), 7: (1, 1)}
+MERGES = {-2: (0, 2), -1: (1, 0), 0: (1, 0), 1: (1, 0), 2: (1, 0), 3: (1, 0), 4: (1, 0), 5: (1, 0), 6: (1, 0), 7: (1, 0)}
 TWICE = (0, 1, 2, 3, 4, 5, 6, 7)
 assert len(ON_TENSOR) * 4 * HALVES * 2 * P * P * N_TILE <= FLOPS // 10
 
@@ -194,8 +195,19 @@ def tile_sindylossmixin_pa_kernel(
         def base_out_of_psum(base, bank, h):
             nc.scalar.activation(out=base[:, half(h)], in_=bank[:], func=COPY, scale=1.0 / 6.0)
 
+        def difference_on_gpsimd(b):
+            base = sums.tile([P, H], F32, name="total")
+            for c in range(0, H, GPSIMD_PIECE):
+                cols = slice(c, c + GPSIMD_PIECE)
+                nc.gpsimd.tensor_tensor(
+                    out=base[:, cols], in0=y_all[:, b, cols], in1=next_all[:, b, cols], op=SUBTRACT
+                )
+            return base
+
         def base_on_vector(b, step, base):
-            if step == 0:
+            if step == 0 and b in DIFFERENCE_ON_GPSIMD:
+                add_scaled(base[:], k1_all[:, b, :], 1.0 / 6.0)
+            elif step == 0:
                 base = sums.tile([P, H], F32, name="total")
                 nc.vector.scalar_tensor_tensor(
                     out=base[:], in0=k1_all[:, b, :], scalar=1.0 / 6.0, in1=next_all[:, b, :],
@@ -215,7 +227,13 @@ def tile_sindylossmixin_pa_kernel(
 
         pairs1, grouped1, grouped2, operand1, operand2 = {}, {}, {}, {}, {}
         doubled_k3, last, total, sixfold, doubled_y = {}, {}, {}, {}, {}
-        waiting = [(b, step) for b in range(B) if b not in ON_TENSOR for step in range(3)]
+        waiting = [
+            (b, step)
+            for b in range(B) if b not in ON_TENSOR
+            for step in range(2 if b in DIFFERENCE_ON_GPSIMD else 3)
+        ]
+        for b in DIFFERENCE_ON_GPSIMD:
+            total[b] = difference_on_gpsimd(b)
 
         served = {"count": 0}
 
@@ -229,33 +247,28 @@ def tile_sindylossmixin_pa_kernel(
         for i in range(FIRST, B + 1):
             if exists(i):
                 grouped2[i] = regroup(turn(second_state(i, doubled_k3[i])), "grouped2")
-            if exists(i + 1):
-                operand1[i + 1] = quantise(grouped1[i + 1], "1")
-            if exists(i) and i in TWICE:
+            if exists(i):
                 last[i] = new_banks()
                 multiply(last[i], operand1[i], True, False)
-            if exists(i + 1):
-                doubled_k3[i + 1] = new_banks()
-                multiply(doubled_k3[i + 1], operand1[i + 1], True, True)
-            merges(MERGES.get(i, (0, 0))[0])
-            if exists(i):
-                operand2[i] = quantise(grouped2[i], "2")
-                if i not in TWICE:
-                    last[i] = new_banks()
-                multiply(last[i], operand2[i], i not in TWICE, True)
-            if exists(i - 1):
-                for h in range(HALVES):
-                    add_scaled(total[i - 1][:, half(h)], last[i - 1][h], 1.0 / 6.0)
-                    nc.sync.dma_start(out=out[i - 1, :, half(h)], in_=total[i - 1][:, half(h)])
-            if exists(i) and i not in TWICE:
-                for h in range(HALVES):
-                    add_scaled(total[i][:, half(h)], doubled_k3[i][h], 1.0 / 6.0)
-            if i + LEAD + 1 in DOUBLED_ON_SCALAR:
-                doubled_y[i + LEAD + 1] = double_y(i + LEAD + 1)
             if exists(i + LEAD):
                 pairs1[i + LEAD] = first_state(i + LEAD)
             if exists(i + 2):
                 grouped1[i + 2] = regroup(turn(pairs1[i + 2]), "grouped1")
+            if exists(i - 1):
+                for h in range(HALVES):
+                    add_scaled(total[i - 1][:, half(h)], last[i - 1][h], 1.0 / 6.0)
+                    nc.sync.dma_start(out=out[i - 1, :, half(h)], in_=total[i - 1][:, half(h)])
+            if exists(i + 1):
+                operand1[i + 1] = quantise(grouped1[i + 1], "1")
+            if exists(i + 1):
+                doubled_k3[i + 1] = new_banks()
+                multiply(doubled_k3[i + 1], operand1[i + 1], True, True)
+            if exists(i):
+                operand2[i] = quantise(grouped2[i], "2")
+                multiply(last[i], operand2[i], False, True)
+            if i + LEAD + 1 in DOUBLED_ON_SCALAR:
+                doubled_y[i + LEAD + 1] = double_y(i + LEAD + 1)
+            merges(MERGES.get(i, (0, 0))[0])
             merges(MERGES.get(i, (0, 0))[1])
             for b in ON_TENSOR:
                 for h in range(HALVES):

@@ -32,7 +32,7 @@ FIRST = -2
 DIFFERENCE_ON_GPSIMD = (1, 3, 5, 7)
 DOUBLED_ON_SCALAR = (2, 3, 4, 5, 6, 7)
 LEAD = 2
-MERGES = {-2: (0, 2), -1: (1, 0), 0: (1, 0), 1: (1, 0), 2: (1, 0), 3: (1, 0), 4: (1, 0), 5: (1, 0), 6: (1, 0), 7: (1, 0)}
+MERGES = {-2: (0, 1), -1: (1, 1), 0: (1, 0), 1: (1, 0), 2: (1, 0), 3: (1, 0), 4: (1, 0), 5: (1, 0), 6: (1, 0), 7: (1, 0)}
 TWICE = (0, 1, 2, 3, 4, 5, 6, 7)
 assert len(ON_TENSOR) * 4 * HALVES * 2 * P * P * N_TILE <= FLOPS // 10
 
@@ -210,20 +210,24 @@ def tile_sindylossmixin_pa_kernel(
             elif step == 0:
                 base = sums.tile([P, H], F32, name="total")
                 nc.vector.scalar_tensor_tensor(
-                    out=base[:], in0=k1_all[:, b, :], scalar=1.0 / 6.0, in1=next_all[:, b, :],
-                    op0=MULT, op1=SUBTRACT,
+                    out=base[:], in0=k2_all[:, b, :], scalar=1.0 / 3.0, in1=y_all[:, b, :], op0=MULT, op1=ADD
                 )
-            elif step == 1:
+            elif step == 1 and b in DIFFERENCE_ON_GPSIMD:
                 add_scaled(base[:], k2_all[:, b, :], 1.0 / 3.0)
+            elif step == 1:
+                add_scaled(base[:], k1_all[:, b, :], 1.0 / 6.0)
             else:
-                add_scaled(base[:], y_all[:, b, :], 1.0)
+                nc.vector.tensor_tensor(out=base[:], in0=base[:], in1=next_all[:, b, :], op=SUBTRACT)
             return base
 
-        for b in range(B):
+        load_state(0)
+        load_state(1)
+        load_w()
+        load_rest(0)
+        load_rest(1)
+        for b in range(2, B):
             load_state(b)
             load_rest(b)
-            if b == 0:
-                load_w()
 
         pairs1, grouped1, grouped2, operand1, operand2 = {}, {}, {}, {}, {}
         doubled_k3, last, total, sixfold, doubled_y = {}, {}, {}, {}, {}

@@ -26,15 +26,17 @@ GPSIMD_PIECE = 256
 
 FLOPS = 2 * 2 * (B * P) * H * H
 
-ON_TENSOR = (2, 4, 6)
-TENSOR_ROUND = {2: 0, 4: 2, 6: 4}
-FIRST = -2
-DIFFERENCE_ON_GPSIMD = (1, 3, 5, 7)
-DOUBLED_ON_SCALAR = (2, 3, 4, 5, 6, 7)
-LEAD = 2
-MERGES = {-2: (0, 1), -1: (1, 1), 0: (1, 0), 1: (1, 0), 2: (1, 0), 3: (1, 0), 4: (1, 0), 5: (1, 0), 6: (1, 0), 7: (1, 0)}
+ON_TENSOR = (0, 2, 4, 5)
+TENSOR_ROUND = {0: ((2, 0),), 1: ((2, 1),), 2: ((4, 0),), 3: ((4, 1),), 4: ((5, 0),), 5: ((5, 1),)}
+DIFFERENCE_ON_GPSIMD = (1, 3, 6, 7)
+DOUBLED_ON_SCALAR = (4, 5, 6, 7)
 TWICE = (0, 1, 2, 3, 4, 5, 6, 7)
-assert len(ON_TENSOR) * 4 * HALVES * 2 * P * P * N_TILE <= FLOPS // 10
+LEAD = 3
+TERM_ORDER = (0, 2, 1)
+MERGES = {0: 0, 1: 2, 2: 1, 3: 1, 4: 1, 5: 2, 6: 1}
+LAST_ROWS = ((0, 5, 2), (5, 6, 1))
+ROW_PARTS = 32
+assert len(ON_TENSOR) * 3 * HALVES * 2 * P * P * N_TILE <= FLOPS // 10
 
 
 def tile_sindylossmixin_pa_kernel(
@@ -52,8 +54,8 @@ def tile_sindylossmixin_pa_kernel(
 
         identity = const.tile([P, P], F32)
         masks.make_identity(nc, identity[:])
-        six_eye = const.tile([P, P], BF16)
-        minus_six_eye = const.tile([P, P], BF16)
+        six_eye = const.tile([P, P], F32)
+        difference = const.tile([P, P], BF16)
         one_eye = const.tile([P, P], BF16)
         two_eye = const.tile([P, P], BF16)
 
@@ -62,14 +64,21 @@ def tile_sindylossmixin_pa_kernel(
         w_scale_words = w_scales[:].bitcast(I32)
         nc.vector.memset(w_scale_words, 0)
         nc.vector.tensor_scalar_mul(out=six_eye[:], in0=identity[:], scalar1=6.0)
-        nc.vector.tensor_scalar_mul(out=minus_six_eye[:], in0=identity[:], scalar1=-6.0)
         nc.vector.tensor_scalar_mul(out=one_eye[:], in0=identity[:], scalar1=1.0)
         nc.vector.tensor_scalar_mul(out=two_eye[:], in0=identity[:], scalar1=2.0)
+        nc.vector.tensor_tensor(
+            out=difference[:, 0 : P - 1], in0=six_eye[:, 0 : P - 1], in1=six_eye[:, 1:P], op=SUBTRACT
+        )
+        nc.vector.tensor_copy(out=difference[:, P - 1 : P], in_=six_eye[:, P - 1 : P])
 
         y_all = inputs.tile([P, B, H], BF16)
         next_all = inputs.tile([P, B, H], BF16)
         k1_all = inputs.tile([P, B, H], BF16)
         k2_all = inputs.tile([P, B, H], BF16)
+        row_words = H // ROW_PARTS
+        last_next = inputs.tile([ROW_PARTS, len(ON_TENSOR), row_words], BF16)
+        last_out = inputs.tile([ROW_PARTS, len(ON_TENSOR), row_words], F32)
+        last_fixed = inputs.tile([ROW_PARTS, len(ON_TENSOR), row_words], F32)
 
         def exists(b):
             return 0 <= b < B
@@ -77,24 +86,53 @@ def tile_sindylossmixin_pa_kernel(
         def half(h):
             return slice(h * N_TILE, (h + 1) * N_TILE)
 
-        def load_w():
+        def load_w_scales():
             for r in range(4):
                 nc.sync.dma_start(
                     out=w_scale_words[r:P:32, :, :],
                     in_=coefficients_scales[:, r:16:4, :].bitcast(I32).rearrange("g q c -> q g c"),
                 )
-            nc.sync.dma_start(
-                out=w_words[:].bitcast(I32),
-                in_=coefficients_words.bitcast(I32).rearrange("g p c -> p g c"),
-            )
+
+        def load_w_words():
+            for g in range(PASSES):
+                nc.sync.dma_start(
+                    out=w_words[:, g, :].bitcast(I32), in_=coefficients_words[g].bitcast(I32)
+                )
+
+        def load_state_half(b, g):
+            nc.sync.dma_start(out=y_all[:, b, half(g)], in_=x[b, 0:P, half(g)])
+            nc.sync.dma_start(out=k2_all[:, b, half(g)], in_=k2[b * P : (b + 1) * P, half(g)])
 
         def load_state(b):
             nc.sync.dma_start(out=y_all[:, b, :], in_=x[b, 0:P, :])
             nc.sync.dma_start(out=k2_all[:, b, :], in_=k2[b * P : (b + 1) * P, :])
 
-        def load_rest(b):
+        def load_k1(b):
             nc.sync.dma_start(out=k1_all[:, b, :], in_=k1[b * P : (b + 1) * P, :])
-            nc.sync.dma_start(out=next_all[:, b, :], in_=x[b, 1 : P + 1, :])
+
+        def load_next(b):
+            if b not in ON_TENSOR:
+                nc.sync.dma_start(out=next_all[:, b, :], in_=x[b, 1 : P + 1, :])
+
+        def spots(start, stop, step):
+            first = ON_TENSOR.index(start)
+            return slice(first, first + len(range(start, stop, step)))
+
+        def load_last_next():
+            for start, stop, step in LAST_ROWS:
+                nc.sync.dma_start(out=last_next[:, spots(start, stop, step), :], in_=spread(x[start:stop:step, P, :]))
+
+        def load_last_out():
+            for start, stop, step in LAST_ROWS:
+                nc.sync.dma_start(out=last_out[:, spots(start, stop, step), :], in_=spread(out[start:stop:step, P - 1, :]))
+
+        def store_last_out():
+            nc.vector.tensor_tensor(out=last_fixed[:], in0=last_out[:], in1=last_next[:], op=SUBTRACT)
+            for start, stop, step in LAST_ROWS:
+                nc.sync.dma_start(out=spread(out[start:stop:step, P - 1, :]), in_=last_fixed[:, spots(start, stop, step), :])
+
+        def spread(rows):
+            return rows.rearrange("b (p c) -> p b c", p=ROW_PARTS)
 
         def first_state(b):
             pairs = operands.tile([P, H], BF16, name="pairs1")
@@ -112,6 +150,18 @@ def tile_sindylossmixin_pa_kernel(
                 )
             return pairs
 
+        def first_state_half(b, pairs, g):
+            for u in range(2):
+                first = u * K_PASS + g * 2 * P
+                nc.vector.scalar_tensor_tensor(
+                    out=pairs[:, first : first + 2 * P].rearrange("m (o p e) -> m o p e", o=1, e=2),
+                    in0=y_all[:, b, half(g)].rearrange("m (p u e) -> m u p e", u=2, e=2)[:, u : u + 1],
+                    scalar=2.0,
+                    in1=k2_all[:, b, half(g)].rearrange("m (p u e) -> m u p e", u=2, e=2)[:, u : u + 1],
+                    op0=MULT,
+                    op1=ADD,
+                )
+
         def double_y(b):
             twice = operands.tile([P, H], BF16, name="twice")
             nc.scalar.activation(out=twice[:], in_=y_all[:, b, :], func=COPY, scale=2.0)
@@ -120,21 +170,60 @@ def tile_sindylossmixin_pa_kernel(
         def second_state(b, doubled_k3):
             pairs = operands.tile([P, H], BF16, name="pairs2")
             for g in range(PASSES):
-                for u in range(2):
-                    first = u * K_PASS + g * 2 * P
-                    nc.vector.scalar_tensor_tensor(
-                        out=pairs[:, first : first + 2 * P].rearrange("m (o p e) -> m o p e", o=1, e=2),
-                        in0=doubled_k3[g].rearrange("m (p u e) -> m u p e", u=2, e=2)[:, u : u + 1],
-                        scalar=0.5,
-                        in1=y_all[:, b, half(g)].rearrange("m (p u e) -> m u p e", u=2, e=2)[:, u : u + 1],
-                        op0=MULT,
-                        op1=ADD,
-                    )
+                second_state_half(b, doubled_k3, pairs, g)
             return pairs
+
+        def second_state_half(b, doubled_k3, pairs, g):
+            for u in range(2):
+                first = u * K_PASS + g * 2 * P
+                nc.vector.scalar_tensor_tensor(
+                    out=pairs[:, first : first + 2 * P].rearrange("m (o p e) -> m o p e", o=1, e=2),
+                    in0=doubled_k3[g].rearrange("m (p u e) -> m u p e", u=2, e=2)[:, u : u + 1],
+                    scalar=0.5,
+                    in1=y_all[:, b, half(g)].rearrange("m (p u e) -> m u p e", u=2, e=2)[:, u : u + 1],
+                    op0=MULT,
+                    op1=ADD,
+                )
+
+        def turn_half(pairs, g):
+            words = pairs[:].bitcast(F32)
+            turned = psum_turned.tile([P, 2 * PASSES, P], F32, name="turned")
+            for u in range(2):
+                first = (u * PASSES + g) * P
+                nc.tensor.transpose(turned[:, u, :], words[:, first : first + P], identity[:])
+            return turned
+
+        def regroup_half(turned, grouped, g):
+            nc.scalar.copy(
+                out=grouped[:, g * K_PASS : (g + 1) * K_PASS].bitcast(F32).rearrange("p (m u) -> p m u", u=2),
+                in_=turned[:, 0:2, :].rearrange("p u m -> p m u"),
+            )
+
+        def quantise_half(grouped, operand, g):
+            codes, scales = operand
+            nc.vector.quantize_mx(
+                out=codes[:, g * P : (g + 1) * P].bitcast(FP8X4),
+                scales=scales[:, g * P : (g + 1) * P],
+                in_=grouped[:, g * K_PASS : (g + 1) * K_PASS],
+            )
+
+        def multiply_half(banks, operand, g, opens, closes):
+            codes, scales = operand
+            rows = slice(g * P, (g + 1) * P)
+            for h in range(HALVES):
+                nc.tensor.matmul_mx(
+                    out=banks[h],
+                    lhsT=codes[:, rows].bitcast(FP8X4),
+                    lhsT_scale=scales[:, rows],
+                    rhs=w_words[:, g, 2 * h * N_TILE : 2 * (h + 1) * N_TILE].bitcast(FP4X4),
+                    rhs_scale=w_scales[:, g, half(h)],
+                    start=opens,
+                    stop=closes,
+                )
 
         def turn(pairs):
             words = pairs[:].bitcast(F32)
-            turned = psum_turned.tile([P, 2 * PASSES, P], F32)
+            turned = psum_turned.tile([P, 2 * PASSES, P], F32, name="turned")
             for g in range(PASSES):
                 for u in range(2):
                     first = (u * PASSES + g) * P
@@ -149,9 +238,13 @@ def tile_sindylossmixin_pa_kernel(
             )
             return grouped
 
-        def quantise(grouped, name):
+        def new_operand(name):
             codes = operands.tile([P, PASSES * P], U32, align_bytes=64, name="codes" + name)
             scales = operands.tile([P, PASSES * P], U8, align_bytes=64, name="scales" + name)
+            return codes, scales
+
+        def quantise(grouped, name):
+            codes, scales = new_operand(name)
             nc.vector.quantize_mx(out=codes[:].bitcast(FP8X4), scales=scales[:], in_=grouped[:])
             return codes, scales
 
@@ -182,102 +275,144 @@ def tile_sindylossmixin_pa_kernel(
                 out=total, in0=term, scalar=factor, in1=total, op0=MULT, op1=ADD
             )
 
-        def base_on_tensor(b, h):
-            terms = ((six_eye, y_all), (minus_six_eye, next_all), (one_eye, k1_all), (two_eye, k2_all))
+        def base_term(b, h, bank, n):
+            eye, source = ((difference, y_all), (one_eye, k1_all), (two_eye, k2_all))[TERM_ORDER[n]]
+            nc.tensor.matmul(out=bank, lhsT=eye[:], rhs=source[:, b, half(h)], start=(n == 0), stop=(n == 2))
+
+        def new_bank():
             bank = psum_banks.tile([P, N_TILE], F32, name="bank")
-            for n, (eye, source) in enumerate(terms):
-                nc.tensor.matmul(
-                    out=bank[:], lhsT=eye[:], rhs=source[:, b, half(h)],
-                    start=(n == 0), stop=(n == len(terms) - 1),
-                )
+            return bank[:]
+
+        def base_on_tensor(b, h):
+            bank = new_bank()
+            for n in range(3):
+                base_term(b, h, bank, n)
             return bank
 
         def base_out_of_psum(base, bank, h):
-            nc.scalar.activation(out=base[:, half(h)], in_=bank[:], func=COPY, scale=1.0 / 6.0)
+            nc.scalar.activation(out=base[:, half(h)], in_=bank, func=COPY, scale=1.0 / 6.0)
 
-        def difference_on_gpsimd(b):
-            base = sums.tile([P, H], F32, name="total")
+        def minus_next_on_gpsimd(b, base, y_or_base):
             for c in range(0, H, GPSIMD_PIECE):
                 cols = slice(c, c + GPSIMD_PIECE)
                 nc.gpsimd.tensor_tensor(
-                    out=base[:, cols], in0=y_all[:, b, cols], in1=next_all[:, b, cols], op=SUBTRACT
+                    out=base[:, cols], in0=y_or_base[:, cols], in1=next_all[:, b, cols], op=SUBTRACT
                 )
-            return base
 
-        def base_on_vector(b, step, base):
-            if step == 0 and b in DIFFERENCE_ON_GPSIMD:
-                add_scaled(base[:], k1_all[:, b, :], 1.0 / 6.0)
-            elif step == 0:
-                base = sums.tile([P, H], F32, name="total")
-                nc.vector.scalar_tensor_tensor(
-                    out=base[:], in0=k2_all[:, b, :], scalar=1.0 / 3.0, in1=y_all[:, b, :], op0=MULT, op1=ADD
-                )
-            elif step == 1 and b in DIFFERENCE_ON_GPSIMD:
-                add_scaled(base[:], k2_all[:, b, :], 1.0 / 3.0)
-            elif step == 1:
-                add_scaled(base[:], k1_all[:, b, :], 1.0 / 6.0)
+        def base_on_vector(b, step):
+            if step == 0:
+                add_scaled(total[b][:], k1_all[:, b, :], 1.0 / 6.0)
             else:
-                nc.vector.tensor_tensor(out=base[:], in0=base[:], in1=next_all[:, b, :], op=SUBTRACT)
-            return base
+                add_scaled(total[b][:], k2_all[:, b, :], 1.0 / 3.0)
 
-        load_state(0)
+        for g in range(PASSES):
+            load_state_half(0, g)
+        load_w_scales()
+        load_w_words()
         load_state(1)
-        load_w()
-        load_rest(0)
-        load_rest(1)
-        for b in range(2, B):
+        load_k1(0)
+        load_state(2)
+        load_k1(2)
+        load_next(1)
+        load_state(3)
+        load_k1(1)
+        load_k1(3)
+        load_next(3)
+        for b in range(4, B):
             load_state(b)
-            load_rest(b)
+            load_k1(b)
+            load_next(b)
+        load_last_next()
 
         pairs1, grouped1, grouped2, operand1, operand2 = {}, {}, {}, {}, {}
         doubled_k3, last, total, sixfold, doubled_y = {}, {}, {}, {}, {}
-        waiting = [
-            (b, step)
-            for b in range(B) if b not in ON_TENSOR
-            for step in range(2 if b in DIFFERENCE_ON_GPSIMD else 3)
-        ]
-        for b in DIFFERENCE_ON_GPSIMD:
-            total[b] = difference_on_gpsimd(b)
-
+        waiting = [(b, step) for b in DIFFERENCE_ON_GPSIMD for step in range(2)]
         served = {"count": 0}
 
         def merges(count):
             for n in range(count):
-                if served["count"] < len(waiting):
-                    b, step = waiting[served["count"]]
-                    served["count"] = served["count"] + 1
-                    total[b] = base_on_vector(b, step, total.get(b))
+                b, step = waiting[served["count"]]
+                served["count"] = served["count"] + 1
+                base_on_vector(b, step)
 
-        for i in range(FIRST, B + 1):
-            if exists(i):
-                grouped2[i] = regroup(turn(second_state(i, doubled_k3[i])), "grouped2")
-            if exists(i):
-                last[i] = new_banks()
-                multiply(last[i], operand1[i], True, False)
-            if exists(i + LEAD):
-                pairs1[i + LEAD] = first_state(i + LEAD)
+        def finish(b, h):
+            add_scaled(total[b][:, half(h)], last[b][h], 1.0 / 6.0)
+            nc.sync.dma_start(out=out[b, :, half(h)], in_=total[b][:, half(h)])
+
+        def evacuate(b, h):
+            if h == 0:
+                total[b] = sums.tile([P, H], F32, name="total")
+            base_out_of_psum(total[b], sixfold[b, h], h)
+
+        def first_round(b):
+            pairs = operands.tile([P, H], BF16, name="pairs1")
+            grouped = operands.tile([P, H], BF16, align_bytes=64, name="grouped1")
+            operand1[b] = new_operand("1")
+            doubled_k3[b] = new_banks()
+            for g in range(PASSES):
+                sixfold[b, g] = new_bank()
+                base_term(b, g, sixfold[b, g], 0)
+                first_state_half(b, pairs, g)
+                regroup_half(turn_half(pairs, g), grouped, g)
+            base_term(b, 0, sixfold[b, 0], 1)
+            for g in range(PASSES):
+                quantise_half(grouped, operand1[b], g)
+                multiply_half(doubled_k3[b], operand1[b], g, g == 0, g == PASSES - 1)
+            base_term(b, 1, sixfold[b, 1], 1)
+
+        def last_round(b):
+            pairs = operands.tile([P, H], BF16, name="pairs2")
+            grouped = operands.tile([P, H], BF16, align_bytes=64, name="grouped2")
+            operand = new_operand("2")
+            last[b] = new_banks()
+            for g in range(PASSES):
+                second_state_half(b, doubled_k3[b], pairs, g)
+                regroup_half(turn_half(pairs, g), grouped, g)
+                multiply_half(last[b], operand1[b], g, g == 0, False)
+            load_last_out()
+            finish(b - 1, 0)
+            for g in range(PASSES):
+                quantise_half(grouped, operand, g)
+                multiply_half(last[b], operand, g, False, g == PASSES - 1)
+            finish(b - 1, 1)
+            store_last_out()
+            for h in range(HALVES):
+                finish(b, h)
+
+        for b in DIFFERENCE_ON_GPSIMD:
+            total[b] = sums.tile([P, H], F32, name="total")
+            minus_next_on_gpsimd(b, total[b], y_all[:, b, :])
+        first_round(0)
+        pairs1[1] = first_state(1)
+        grouped1[1] = regroup(turn(pairs1[1]), "grouped1")
+        for h in range(HALVES):
+            base_term(0, h, sixfold[0, h], 2)
+        for i in range(B - 1):
+            pairs2 = second_state(i, doubled_k3[i])
+            for b, h in TENSOR_ROUND.get(i, ()):
+                sixfold[b, h] = base_on_tensor(b, h)
+            grouped2[i] = regroup(turn(pairs2), "grouped2")
+            if i == 0:
+                pairs1[2] = first_state(2)
             if exists(i + 2):
                 grouped1[i + 2] = regroup(turn(pairs1[i + 2]), "grouped1")
+            for b, h in (((0, 0), (0, 1)) if i == 0 else ()) + TENSOR_ROUND.get(i, ()):
+                evacuate(b, h)
+            last[i] = new_banks()
+            multiply(last[i], operand1[i], True, False)
             if exists(i - 1):
                 for h in range(HALVES):
-                    add_scaled(total[i - 1][:, half(h)], last[i - 1][h], 1.0 / 6.0)
-                    nc.sync.dma_start(out=out[i - 1, :, half(h)], in_=total[i - 1][:, half(h)])
-            if exists(i + 1):
-                operand1[i + 1] = quantise(grouped1[i + 1], "1")
-            if exists(i + 1):
-                doubled_k3[i + 1] = new_banks()
-                multiply(doubled_k3[i + 1], operand1[i + 1], True, True)
-            if exists(i):
-                operand2[i] = quantise(grouped2[i], "2")
-                multiply(last[i], operand2[i], False, True)
+                    finish(i - 1, h)
+            if i > 0 and exists(i + LEAD):
+                pairs1[i + LEAD] = first_state(i + LEAD)
+            operand1[i + 1] = quantise(grouped1[i + 1], "1")
+            doubled_k3[i + 1] = new_banks()
+            multiply(doubled_k3[i + 1], operand1[i + 1], True, True)
+            operand2[i] = quantise(grouped2[i], "2")
+            multiply(last[i], operand2[i], False, True)
             if i + LEAD + 1 in DOUBLED_ON_SCALAR:
                 doubled_y[i + LEAD + 1] = double_y(i + LEAD + 1)
-            merges(MERGES.get(i, (0, 0))[0])
-            merges(MERGES.get(i, (0, 0))[1])
-            for b in ON_TENSOR:
-                for h in range(HALVES):
-                    if TENSOR_ROUND[b] + h == i:
-                        sixfold[b, h] = base_on_tensor(b, h)
-                        if h == 0:
-                            total[b] = sums.tile([P, H], F32, name="total")
-                        base_out_of_psum(total[b], sixfold[b, h], h)
+            if i == 0:
+                pairs1[LEAD] = first_state(LEAD)
+            merges(MERGES[i])
+        last_round(B - 1)

@@ -22,18 +22,15 @@ K_PASS = 512
 PASSES = H // K_PASS
 N_TILE = 512
 HALVES = H // N_TILE
-GPSIMD_PIECE = 256
 
 FLOPS = 2 * 2 * (B * P) * H * H
 
 ON_TENSOR = (0, 2, 4, 5)
-TENSOR_ROUND = {0: ((2, 0),), 1: ((2, 1),), 2: ((4, 0),), 3: ((4, 1),), 4: ((5, 0),), 5: ((5, 1),)}
-DIFFERENCE_ON_GPSIMD = (1, 3, 6, 7)
+TENSOR_ROUND = {1: ((2, 0),), 2: ((2, 1),), 3: ((4, 0),), 4: ((4, 1), (5, 0)), 5: ((5, 1),)}
 DOUBLED_ON_SCALAR = (4, 5, 6, 7)
-TWICE = (0, 1, 2, 3, 4, 5, 6, 7)
 LEAD = 3
 TERM_ORDER = (0, 2, 1)
-MERGES = {0: 0, 1: 2, 2: 1, 3: 1, 4: 1, 5: 2, 6: 1}
+MERGES = {0: ((1, 0),), 1: ((1, 1),), 2: ((3, 0),), 3: ((3, 1),), 4: ((6, 0),), 5: ((6, 1), (7, 0)), 6: ((7, 1),)}
 LAST_ROWS = ((0, 5, 2), (5, 6, 1))
 ROW_PARTS = 32
 assert len(ON_TENSOR) * 3 * HALVES * 2 * P * P * N_TILE <= FLOPS // 10
@@ -127,7 +124,7 @@ def tile_sindylossmixin_pa_kernel(
                 nc.sync.dma_start(out=last_out[:, spots(start, stop, step), :], in_=spread(out[start:stop:step, P - 1, :]))
 
         def store_last_out():
-            nc.vector.tensor_tensor(out=last_fixed[:], in0=last_out[:], in1=last_next[:], op=SUBTRACT)
+            nc.gpsimd.tensor_tensor(out=last_fixed[:], in0=last_out[:], in1=last_next[:], op=SUBTRACT)
             for start, stop, step in LAST_ROWS:
                 nc.sync.dma_start(out=spread(out[start:stop:step, P - 1, :]), in_=last_fixed[:, spots(start, stop, step), :])
 
@@ -136,18 +133,13 @@ def tile_sindylossmixin_pa_kernel(
 
         def first_state(b):
             pairs = operands.tile([P, H], BF16, name="pairs1")
-            if b in DOUBLED_ON_SCALAR:
-                twice = doubled_y[b]
-            else:
-                twice = operands.tile([P, H], BF16, name="twice")
-                nc.vector.tensor_scalar_mul(out=twice[:], in0=y_all[:, b, :], scalar1=2.0)
-            for u in range(2):
-                nc.vector.tensor_tensor(
-                    out=pairs[:, u * K_PASS : (u + 1) * K_PASS].rearrange("m (o q e) -> m o q e", o=1, e=2),
-                    in0=twice[:].rearrange("m (q u e) -> m u q e", u=2, e=2)[:, u : u + 1],
-                    in1=k2_all[:, b, :].rearrange("m (q u e) -> m u q e", u=2, e=2)[:, u : u + 1],
-                    op=ADD,
-                )
+            twice = doubled_y[b]
+            nc.vector.tensor_tensor(
+                out=pairs[:].rearrange("m (u q e) -> m u q e", u=2, e=2),
+                in0=twice[:].rearrange("m (q u e) -> m u q e", u=2, e=2),
+                in1=k2_all[:, b, :].rearrange("m (q u e) -> m u q e", u=2, e=2),
+                op=ADD,
+            )
             return pairs
 
         def first_state_half(b, pairs, g):
@@ -161,6 +153,11 @@ def tile_sindylossmixin_pa_kernel(
                     op0=MULT,
                     op1=ADD,
                 )
+
+        def double_on_vector(b):
+            twice = operands.tile([P, H], BF16, name="twice")
+            nc.vector.tensor_scalar_mul(out=twice[:], in0=y_all[:, b, :], scalar1=2.0)
+            return twice
 
         def double_y(b):
             twice = operands.tile([P, H], BF16, name="twice")
@@ -292,18 +289,21 @@ def tile_sindylossmixin_pa_kernel(
         def base_out_of_psum(base, bank, h):
             nc.scalar.activation(out=base[:, half(h)], in_=bank, func=COPY, scale=1.0 / 6.0)
 
-        def minus_next_on_gpsimd(b, base, y_or_base):
-            for c in range(0, H, GPSIMD_PIECE):
-                cols = slice(c, c + GPSIMD_PIECE)
-                nc.gpsimd.tensor_tensor(
-                    out=base[:, cols], in0=y_or_base[:, cols], in1=next_all[:, b, cols], op=SUBTRACT
-                )
+        def minus_next(b):
+            nc.gpsimd.tensor_tensor(out=total[b][:], in0=total[b][:], in1=next_all[:, b, :], op=SUBTRACT)
 
-        def base_on_vector(b, step):
+        def k2_and_y(b):
+            total[b] = sums.tile([P, H], F32, name="total")
+            nc.vector.scalar_tensor_tensor(
+                out=total[b][:], in0=k2_all[:, b, :], scalar=1.0 / 3.0, in1=y_all[:, b, :], op0=MULT, op1=ADD
+            )
+
+        def merge(b, step):
             if step == 0:
-                add_scaled(total[b][:], k1_all[:, b, :], 1.0 / 6.0)
+                k2_and_y(b)
+                minus_next(b)
             else:
-                add_scaled(total[b][:], k2_all[:, b, :], 1.0 / 3.0)
+                add_scaled(total[b][:], k1_all[:, b, :], 1.0 / 6.0)
 
         for g in range(PASSES):
             load_state_half(0, g)
@@ -312,9 +312,9 @@ def tile_sindylossmixin_pa_kernel(
         load_state(1)
         load_k1(0)
         load_state(2)
+        load_state(3)
         load_k1(2)
         load_next(1)
-        load_state(3)
         load_k1(1)
         load_k1(3)
         load_next(3)
@@ -326,14 +326,6 @@ def tile_sindylossmixin_pa_kernel(
 
         pairs1, grouped1, grouped2, operand1, operand2 = {}, {}, {}, {}, {}
         doubled_k3, last, total, sixfold, doubled_y = {}, {}, {}, {}, {}
-        waiting = [(b, step) for b in DIFFERENCE_ON_GPSIMD for step in range(2)]
-        served = {"count": 0}
-
-        def merges(count):
-            for n in range(count):
-                b, step = waiting[served["count"]]
-                served["count"] = served["count"] + 1
-                base_on_vector(b, step)
 
         def finish(b, h):
             add_scaled(total[b][:, half(h)], last[b][h], 1.0 / 6.0)
@@ -343,6 +335,11 @@ def tile_sindylossmixin_pa_kernel(
             if h == 0:
                 total[b] = sums.tile([P, H], F32, name="total")
             base_out_of_psum(total[b], sixfold[b, h], h)
+
+        def start_next(b):
+            operand1[b] = quantise(grouped1[b], "1")
+            doubled_k3[b] = new_banks()
+            multiply(doubled_k3[b], operand1[b], True, True)
 
         def first_round(b):
             pairs = operands.tile([P, H], BF16, name="pairs1")
@@ -379,40 +376,46 @@ def tile_sindylossmixin_pa_kernel(
             for h in range(HALVES):
                 finish(b, h)
 
-        for b in DIFFERENCE_ON_GPSIMD:
-            total[b] = sums.tile([P, H], F32, name="total")
-            minus_next_on_gpsimd(b, total[b], y_all[:, b, :])
         first_round(0)
+        doubled_y[1] = double_on_vector(1)
         pairs1[1] = first_state(1)
         grouped1[1] = regroup(turn(pairs1[1]), "grouped1")
         for h in range(HALVES):
             base_term(0, h, sixfold[0, h], 2)
+        evacuate(0, 0)
         for i in range(B - 1):
             pairs2 = second_state(i, doubled_k3[i])
             for b, h in TENSOR_ROUND.get(i, ()):
                 sixfold[b, h] = base_on_tensor(b, h)
+            if i == 0:
+                doubled_y[2] = double_on_vector(2)
             grouped2[i] = regroup(turn(pairs2), "grouped2")
             if i == 0:
+                evacuate(0, 1)
+                start_next(1)
                 pairs1[2] = first_state(2)
+                doubled_y[3] = double_on_vector(3)
+            if i == 1:
+                pairs1[3] = first_state(3)
             if exists(i + 2):
                 grouped1[i + 2] = regroup(turn(pairs1[i + 2]), "grouped1")
-            for b, h in (((0, 0), (0, 1)) if i == 0 else ()) + TENSOR_ROUND.get(i, ()):
+            for b, h in TENSOR_ROUND.get(i, ()):
                 evacuate(b, h)
             last[i] = new_banks()
             multiply(last[i], operand1[i], True, False)
             if exists(i - 1):
                 for h in range(HALVES):
                     finish(i - 1, h)
-            if i > 0 and exists(i + LEAD):
+            if i > 1 and exists(i + LEAD):
                 pairs1[i + LEAD] = first_state(i + LEAD)
-            operand1[i + 1] = quantise(grouped1[i + 1], "1")
-            doubled_k3[i + 1] = new_banks()
-            multiply(doubled_k3[i + 1], operand1[i + 1], True, True)
+            if i > 0:
+                start_next(i + 1)
             operand2[i] = quantise(grouped2[i], "2")
             multiply(last[i], operand2[i], False, True)
             if i + LEAD + 1 in DOUBLED_ON_SCALAR:
                 doubled_y[i + LEAD + 1] = double_y(i + LEAD + 1)
-            if i == 0:
-                pairs1[LEAD] = first_state(LEAD)
-            merges(MERGES[i])
+            if i == 1:
+                pairs1[4] = first_state(4)
+            for b, step in MERGES[i]:
+                merge(b, step)
         last_round(B - 1)

@@ -25,13 +25,15 @@ HALVES = H // N_TILE
 
 FLOPS = 2 * 2 * (B * P) * H * H
 
-ON_TENSOR = (0, 2, 4, 5)
-TENSOR_ROUND = {1: ((2, 0),), 2: ((2, 1),), 3: ((4, 0),), 4: ((4, 1), (5, 0)), 5: ((5, 1),)}
+ON_TENSOR = (0, 1, 2, 4)
+TENSOR_ROUND = {0: ((1, 0),), 1: ((1, 1),), 2: ((2, 0), (2, 1)), 3: ((4, 0),), 4: ((4, 1),)}
 DOUBLED_ON_SCALAR = (4, 5, 6, 7)
 LEAD = 3
 TERM_ORDER = (0, 2, 1)
-MERGES = {0: ((1, 0),), 1: ((1, 1),), 2: ((3, 0),), 3: ((3, 1),), 4: ((6, 0),), 5: ((6, 1), (7, 0)), 6: ((7, 1),)}
-LAST_ROWS = ((0, 5, 2), (5, 6, 1))
+MERGES = {0: ("k2 and y", 3), 2: ("k2 and y", 5), 4: ("k2 and y", 6), 5: ("k2 and y", 7), 6: ("k1", 6)}
+GPSIMD_ROUND = {1: ("next", 3), 2: ("k1", 3), 3: ("next", 5), 4: ("k1", 5), 5: ("next", 6), 6: ("next", 7), 7: ("k1", 7)}
+UNDOUBLED = (1, 3)
+LAST_ROWS = ((0, 3, 1), (4, 5, 1))
 ROW_PARTS = 32
 assert len(ON_TENSOR) * 3 * HALVES * 2 * P * P * N_TILE <= FLOPS // 10
 
@@ -75,6 +77,8 @@ def tile_sindylossmixin_pa_kernel(
         row_words = H // ROW_PARTS
         last_next = inputs.tile([ROW_PARTS, len(ON_TENSOR), row_words], BF16)
         last_out = inputs.tile([ROW_PARTS, len(ON_TENSOR), row_words], F32)
+        sync_f32 = inputs.tile([P, B], F32)
+        sync_u32 = inputs.tile([P, B], U32)
         last_fixed = inputs.tile([ROW_PARTS, len(ON_TENSOR), row_words], F32)
 
         def exists(b):
@@ -298,12 +302,29 @@ def tile_sindylossmixin_pa_kernel(
                 out=total[b][:], in0=k2_all[:, b, :], scalar=1.0 / 3.0, in1=y_all[:, b, :], op0=MULT, op1=ADD
             )
 
-        def merge(b, step):
-            if step == 0:
+        def merge(i):
+            what, b = MERGES.get(i, ("", 0))
+            if what == "k2 and y":
                 k2_and_y(b)
-                minus_next(b)
-            else:
+            elif what == "k1":
                 add_scaled(total[b][:], k1_all[:, b, :], 1.0 / 6.0)
+
+        def merge_on_gpsimd(i):
+            what, b = GPSIMD_ROUND.get(i, ("", 0))
+            if what == "next":
+                minus_next(b)
+            elif what == "k1":
+                if i - 1 in UNDOUBLED:
+                    nc.gpsimd.tensor_copy(out=sync_f32[:, i : i + 1], in_=total[i - 1][:, H - 1 : H])
+                elif i - 1 in MERGES:
+                    nc.gpsimd.tensor_copy(out=sync_f32[:, i : i + 1], in_=total[MERGES[i - 1][1]][:, 0:1])
+                else:
+                    nc.gpsimd.tensor_copy(out=sync_u32[:, i : i + 1], in_=operand2[i - 1][0][:, 0:1])
+                nc.gpsimd.tensor_tensor(out=total[b][:], in0=total[b][:], in1=sixth[b][:], op=ADD)
+
+        def sixth_of_k1(b):
+            sixth[b] = operands.tile([P, H], F32, name="sixth")
+            nc.scalar.activation(out=sixth[b][:], in_=k1_all[:, b, :], func=COPY, scale=1.0 / 6.0)
 
         for g in range(PASSES):
             load_state_half(0, g)
@@ -312,12 +333,11 @@ def tile_sindylossmixin_pa_kernel(
         load_state(1)
         load_k1(0)
         load_state(2)
-        load_state(3)
-        load_k1(2)
-        load_next(1)
         load_k1(1)
-        load_k1(3)
+        load_state(3)
         load_next(3)
+        load_k1(2)
+        load_k1(3)
         for b in range(4, B):
             load_state(b)
             load_k1(b)
@@ -326,6 +346,7 @@ def tile_sindylossmixin_pa_kernel(
 
         pairs1, grouped1, grouped2, operand1, operand2 = {}, {}, {}, {}, {}
         doubled_k3, last, total, sixfold, doubled_y = {}, {}, {}, {}, {}
+        sixth = {}
 
         def finish(b, h):
             add_scaled(total[b][:, half(h)], last[b][h], 1.0 / 6.0)
@@ -340,6 +361,16 @@ def tile_sindylossmixin_pa_kernel(
             operand1[b] = quantise(grouped1[b], "1")
             doubled_k3[b] = new_banks()
             multiply(doubled_k3[b], operand1[b], True, True)
+
+        def double(b):
+            if b not in UNDOUBLED:
+                last[b] = new_banks()
+                multiply(last[b], operand1[b], True, False)
+
+        def add_k3(b):
+            if b in UNDOUBLED:
+                for h in range(HALVES):
+                    add_scaled(total[b][:, half(h)], doubled_k3[b][h], 1.0 / 6.0)
 
         def first_round(b):
             pairs = operands.tile([P, H], BF16, name="pairs1")
@@ -365,12 +396,14 @@ def tile_sindylossmixin_pa_kernel(
             for g in range(PASSES):
                 second_state_half(b, doubled_k3[b], pairs, g)
                 regroup_half(turn_half(pairs, g), grouped, g)
-                multiply_half(last[b], operand1[b], g, g == 0, False)
+                if b not in UNDOUBLED:
+                    multiply_half(last[b], operand1[b], g, g == 0, False)
+            merge_on_gpsimd(b)
             load_last_out()
             finish(b - 1, 0)
             for g in range(PASSES):
                 quantise_half(grouped, operand, g)
-                multiply_half(last[b], operand, g, False, g == PASSES - 1)
+                multiply_half(last[b], operand, g, b in UNDOUBLED and g == 0, g == PASSES - 1)
             finish(b - 1, 1)
             store_last_out()
             for h in range(HALVES):
@@ -385,6 +418,7 @@ def tile_sindylossmixin_pa_kernel(
         evacuate(0, 0)
         for i in range(B - 1):
             pairs2 = second_state(i, doubled_k3[i])
+            merge_on_gpsimd(i)
             for b, h in TENSOR_ROUND.get(i, ()):
                 sixfold[b, h] = base_on_tensor(b, h)
             if i == 0:
@@ -401,8 +435,9 @@ def tile_sindylossmixin_pa_kernel(
                 grouped1[i + 2] = regroup(turn(pairs1[i + 2]), "grouped1")
             for b, h in TENSOR_ROUND.get(i, ()):
                 evacuate(b, h)
-            last[i] = new_banks()
-            multiply(last[i], operand1[i], True, False)
+            if GPSIMD_ROUND.get(i + 1, ("", 0))[0] == "k1":
+                sixth_of_k1(GPSIMD_ROUND[i + 1][1])
+            double(i)
             if exists(i - 1):
                 for h in range(HALVES):
                     finish(i - 1, h)
@@ -411,11 +446,13 @@ def tile_sindylossmixin_pa_kernel(
             if i > 0:
                 start_next(i + 1)
             operand2[i] = quantise(grouped2[i], "2")
-            multiply(last[i], operand2[i], False, True)
+            if i in UNDOUBLED:
+                last[i] = new_banks()
+            multiply(last[i], operand2[i], i in UNDOUBLED, True)
             if i + LEAD + 1 in DOUBLED_ON_SCALAR:
                 doubled_y[i + LEAD + 1] = double_y(i + LEAD + 1)
             if i == 1:
                 pairs1[4] = first_state(4)
-            for b, step in MERGES[i]:
-                merge(b, step)
+            merge(i)
+            add_k3(i)
         last_round(B - 1)

@@ -25,15 +25,18 @@ HALVES = H // N_TILE
 
 FLOPS = 2 * 2 * (B * P) * H * H
 
-ON_TENSOR = (0, 1, 2, 4)
-TENSOR_ROUND = {0: ((1, 0),), 1: ((1, 1),), 2: ((2, 0), (2, 1)), 3: ((4, 0),), 4: ((4, 1),)}
-DOUBLED_ON_SCALAR = (4, 5, 6, 7)
+ON_TENSOR = (0, 2, 3, 4)
+TENSOR_ROUND = {0: ((2, 0),), 1: ((2, 1),), 2: ((3, 0),), 3: ((3, 1),), 4: ((4, 0),), 5: ((4, 1),)}
+DOUBLED_ON_SCALAR = (5, 6, 7)
 LEAD = 3
+ORDERS = {0: "s2 t2 s1a t1 base0 dv3 dbl m q2 k4 base ev", 1: "s2 dv4 t2 s1b t1 base ev s1 dy q1 k3 dbl m q2 g k4 fin", 2: "s2 base ev t2 t1 s1 sx dy q1 k3 dbl add m q2 g k4 fin", 3: "s2 base ev t2 t1 s1 sx dy q1 k3 dbl add m q2 g k4 fin", 4: "s2 base ev t2 t1 s1 sx dy q1 k3 dbl add m q2 g k4 fin", 5: "s2 base ev t2 t1 s1 sx dy q1 k3 dbl add m q2 q7 g k4 fin k7", 6: "s2 t2 fin sx dbl s7a t7a s7b t7b q2 k4 add7"}
 TERM_ORDER = (0, 2, 1)
-MERGES = {0: ("k2 and y", 3), 2: ("k2 and y", 5), 4: ("k2 and y", 6), 5: ("k2 and y", 7), 6: ("k1", 6)}
-GPSIMD_ROUND = {1: ("next", 3), 2: ("k1", 3), 3: ("next", 5), 4: ("k1", 5), 5: ("next", 6), 6: ("next", 7), 7: ("k1", 7)}
-UNDOUBLED = (1, 3)
-LAST_ROWS = ((0, 3, 1), (4, 5, 1))
+MERGES = {-1: ("k2 and y", 1), 0: ("k1", 1), 1: ("k2 and y", 5), 2: ("k2 and y", 6), 3: ("k2 and y", 7), 4: ("k1", 6), 5: ("k1", 7)}
+GPSIMD_ROUND = {2: ("next", 1), 3: ("next", 5), 4: ("k1", 5), 5: ("next", 6), 6: ("next", 7)}
+UNDOUBLED = (7,)
+MERGES2 = {}
+SIXTH_ROUND = {2: 5}
+LAST_ROWS = ((0, 1, 1), (2, 5, 1))
 ROW_PARTS = 32
 assert len(ON_TENSOR) * 3 * HALVES * 2 * P * P * N_TILE <= FLOPS // 10
 
@@ -296,30 +299,27 @@ def tile_sindylossmixin_pa_kernel(
         def minus_next(b):
             nc.gpsimd.tensor_tensor(out=total[b][:], in0=total[b][:], in1=next_all[:, b, :], op=SUBTRACT)
 
-        def k2_and_y(b):
-            total[b] = sums.tile([P, H], F32, name="total")
-            nc.vector.scalar_tensor_tensor(
-                out=total[b][:], in0=k2_all[:, b, :], scalar=1.0 / 3.0, in1=y_all[:, b, :], op0=MULT, op1=ADD
-            )
-
-        def merge(i):
-            what, b = MERGES.get(i, ("", 0))
+        def merge(i, h, table):
+            what, b = table.get(i, ("", 0))
             if what == "k2 and y":
-                k2_and_y(b)
+                if h == 0:
+                    total[b] = sums.tile([P, H], F32, name="total")
+                nc.vector.scalar_tensor_tensor(
+                    out=total[b][:, half(h)], in0=k2_all[:, b, half(h)], scalar=1.0 / 3.0,
+                    in1=y_all[:, b, half(h)], op0=MULT, op1=ADD,
+                )
             elif what == "k1":
-                add_scaled(total[b][:], k1_all[:, b, :], 1.0 / 6.0)
+                add_scaled(total[b][:, half(h)], k1_all[:, b, half(h)], 1.0 / 6.0)
 
         def merge_on_gpsimd(i):
             what, b = GPSIMD_ROUND.get(i, ("", 0))
             if what == "next":
                 minus_next(b)
             elif what == "k1":
-                if i - 1 in UNDOUBLED:
-                    nc.gpsimd.tensor_copy(out=sync_f32[:, i : i + 1], in_=total[i - 1][:, H - 1 : H])
-                elif i - 1 in MERGES:
-                    nc.gpsimd.tensor_copy(out=sync_f32[:, i : i + 1], in_=total[MERGES[i - 1][1]][:, 0:1])
-                else:
-                    nc.gpsimd.tensor_copy(out=sync_u32[:, i : i + 1], in_=operand2[i - 1][0][:, 0:1])
+                if i - 1 in MERGES:
+                    nc.gpsimd.tensor_copy(out=sync_f32[:, i : i + 1], in_=total[MERGES[i - 1][1]][:, H - 1 : H])
+                elif i in operand1:
+                    nc.gpsimd.tensor_copy(out=sync_u32[:, i : i + 1], in_=operand1[i][0][:, 0:1])
                 nc.gpsimd.tensor_tensor(out=total[b][:], in0=total[b][:], in1=sixth[b][:], op=ADD)
 
         def sixth_of_k1(b):
@@ -328,15 +328,15 @@ def tile_sindylossmixin_pa_kernel(
 
         for g in range(PASSES):
             load_state_half(0, g)
+        load_state(1)
         load_w_scales()
         load_w_words()
-        load_state(1)
-        load_k1(0)
         load_state(2)
-        load_k1(1)
-        load_state(3)
-        load_next(3)
+        load_k1(0)
         load_k1(2)
+        load_state(3)
+        load_next(1)
+        load_k1(1)
         load_k1(3)
         for b in range(4, B):
             load_state(b)
@@ -372,87 +372,187 @@ def tile_sindylossmixin_pa_kernel(
                 for h in range(HALVES):
                     add_scaled(total[b][:, half(h)], doubled_k3[b][h], 1.0 / 6.0)
 
-        def first_round(b):
-            pairs = operands.tile([P, H], BF16, name="pairs1")
-            grouped = operands.tile([P, H], BF16, align_bytes=64, name="grouped1")
-            operand1[b] = new_operand("1")
+        pairs2 = {}
+
+        def s2(i, g=None):
+            if g is None:
+                pairs2[i] = second_state(i, doubled_k3[i])
+            else:
+                if g == 0:
+                    pairs2[i] = operands.tile([P, H], BF16, name="pairs2")
+                second_state_half(i, doubled_k3[i], pairs2[i], g)
+
+        def t2(i, g=None):
+            if g is None:
+                grouped2[i] = regroup(turn(pairs2[i]), "grouped2")
+            else:
+                if g == 0:
+                    grouped2[i] = operands.tile([P, H], BF16, align_bytes=64, name="grouped2")
+                regroup_half(turn_half(pairs2[i], g), grouped2[i], g)
+
+        def t1(b):
+            if exists(b):
+                grouped1[b] = regroup(turn(pairs1[b]), "grouped1")
+
+        def q1(b):
+            operand1[b] = quantise(grouped1[b], "1")
+
+        def k3(b):
             doubled_k3[b] = new_banks()
-            for g in range(PASSES):
-                sixfold[b, g] = new_bank()
-                base_term(b, g, sixfold[b, g], 0)
-                first_state_half(b, pairs, g)
-                regroup_half(turn_half(pairs, g), grouped, g)
-            base_term(b, 0, sixfold[b, 0], 1)
-            for g in range(PASSES):
-                quantise_half(grouped, operand1[b], g)
-                multiply_half(doubled_k3[b], operand1[b], g, g == 0, g == PASSES - 1)
-            base_term(b, 1, sixfold[b, 1], 1)
+            multiply(doubled_k3[b], operand1[b], True, True)
 
-        def last_round(b):
-            pairs = operands.tile([P, H], BF16, name="pairs2")
-            grouped = operands.tile([P, H], BF16, align_bytes=64, name="grouped2")
-            operand = new_operand("2")
-            last[b] = new_banks()
-            for g in range(PASSES):
-                second_state_half(b, doubled_k3[b], pairs, g)
-                regroup_half(turn_half(pairs, g), grouped, g)
-                if b not in UNDOUBLED:
-                    multiply_half(last[b], operand1[b], g, g == 0, False)
-            merge_on_gpsimd(b)
-            load_last_out()
-            finish(b - 1, 0)
-            for g in range(PASSES):
-                quantise_half(grouped, operand, g)
-                multiply_half(last[b], operand, g, b in UNDOUBLED and g == 0, g == PASSES - 1)
-            finish(b - 1, 1)
-            store_last_out()
-            for h in range(HALVES):
-                finish(b, h)
+        def q2(i, g=None):
+            if g is None:
+                operand2[i] = quantise(grouped2[i], "2")
+            else:
+                if g == 0:
+                    operand2[i] = new_operand("2")
+                quantise_half(grouped2[i], operand2[i], g)
 
-        first_round(0)
-        doubled_y[1] = double_on_vector(1)
-        pairs1[1] = first_state(1)
-        grouped1[1] = regroup(turn(pairs1[1]), "grouped1")
-        for h in range(HALVES):
-            base_term(0, h, sixfold[0, h], 2)
-        evacuate(0, 0)
-        for i in range(B - 1):
-            pairs2 = second_state(i, doubled_k3[i])
-            merge_on_gpsimd(i)
+        def k4(i, g=None):
+            if i in UNDOUBLED and not g:
+                last[i] = new_banks()
+            if g is None:
+                multiply(last[i], operand2[i], i in UNDOUBLED, True)
+            else:
+                multiply_half(last[i], operand2[i], g, i in UNDOUBLED and g == 0, g == PASSES - 1)
+
+        def s1(b):
+            if exists(b):
+                pairs1[b] = first_state(b)
+
+        def fin(b, h=None):
+            if exists(b):
+                for n in range(HALVES) if h is None else (h,):
+                    finish(b, n)
+
+        def base(i):
             for b, h in TENSOR_ROUND.get(i, ()):
                 sixfold[b, h] = base_on_tensor(b, h)
-            if i == 0:
-                doubled_y[2] = double_on_vector(2)
-            grouped2[i] = regroup(turn(pairs2), "grouped2")
-            if i == 0:
-                evacuate(0, 1)
-                start_next(1)
-                pairs1[2] = first_state(2)
-                doubled_y[3] = double_on_vector(3)
-            if i == 1:
-                pairs1[3] = first_state(3)
-            if exists(i + 2):
-                grouped1[i + 2] = regroup(turn(pairs1[i + 2]), "grouped1")
+
+        def ev(i):
             for b, h in TENSOR_ROUND.get(i, ()):
                 evacuate(b, h)
-            if GPSIMD_ROUND.get(i + 1, ("", 0))[0] == "k1":
-                sixth_of_k1(GPSIMD_ROUND[i + 1][1])
-            double(i)
-            if exists(i - 1):
-                for h in range(HALVES):
-                    finish(i - 1, h)
-            if i > 1 and exists(i + LEAD):
-                pairs1[i + LEAD] = first_state(i + LEAD)
-            if i > 0:
-                start_next(i + 1)
-            operand2[i] = quantise(grouped2[i], "2")
-            if i in UNDOUBLED:
-                last[i] = new_banks()
-            multiply(last[i], operand2[i], i in UNDOUBLED, True)
-            if i + LEAD + 1 in DOUBLED_ON_SCALAR:
-                doubled_y[i + LEAD + 1] = double_y(i + LEAD + 1)
-            if i == 1:
-                pairs1[4] = first_state(4)
-            merge(i)
-            add_k3(i)
-        last_round(B - 1)
+
+        def sx(i):
+            if i in SIXTH_ROUND:
+                sixth_of_k1(SIXTH_ROUND[i])
+
+        def dy(b):
+            if b in DOUBLED_ON_SCALAR:
+                doubled_y[b] = double_y(b)
+
+        def dv(b):
+            doubled_y[b] = double_on_vector(b)
+
+        def run(order, i):
+            for step in order.split():
+                if step == "q1":
+                    q1(i + 1)
+                elif step == "k3":
+                    k3(i + 1)
+                elif step == "s2":
+                    s2(i)
+                elif step == "t2":
+                    t2(i)
+                elif step == "t1":
+                    t1(i + 2)
+                elif step == "fin":
+                    fin(i - 1)
+                elif step == "dbl":
+                    double(i)
+                elif step == "base":
+                    base(i)
+                elif step == "ev":
+                    ev(i)
+                elif step == "s1":
+                    s1(i + LEAD)
+                elif step == "add":
+                    add_k3(i)
+                elif step == "ma":
+                    merge(i, 0, MERGES)
+                elif step == "mb":
+                    merge(i, 1, MERGES)
+                elif step == "na":
+                    merge(i, 0, MERGES2)
+                elif step == "nb":
+                    merge(i, 1, MERGES2)
+                elif step == "q2":
+                    q2(i)
+                elif step == "k4":
+                    k4(i)
+                elif step == "sx":
+                    sx(i)
+                elif step == "dy":
+                    dy(i + LEAD + 1)
+                elif step == "s1a":
+                    s1(2)
+                elif step == "s1b":
+                    s1(3)
+                elif step == "dv4":
+                    dv(4)
+                elif step == "dv3":
+                    dv(3)
+                elif step == "base0":
+                    for h in range(HALVES):
+                        base_term(0, h, sixfold[0, h], 2)
+                        evacuate(0, h)
+                elif step == "q7":
+                    q1(7)
+                elif step == "k7":
+                    k3(7)
+                elif step == "add7":
+                    add_k3(7)
+                elif step == "s7a":
+                    s2(7, 0)
+                elif step == "t7a":
+                    t2(7, 0)
+                elif step == "s7b":
+                    s2(7, 1)
+                elif step == "t7b":
+                    t2(7, 1)
+                elif step == "f6":
+                    fin(6)
+                elif step == "s7":
+                    for g in range(PASSES):
+                        s2(7, g)
+                        t2(7, g)
+                elif step == "dbl7":
+                    double(7)
+                elif step == "g":
+                    merge_on_gpsimd(i + 1)
+                elif step == "m":
+                    merge(i, 0, MERGES)
+                    merge(i, 1, MERGES)
+
+        pairs1[0] = operands.tile([P, H], BF16, name="pairs1")
+        grouped1[0] = operands.tile([P, H], BF16, align_bytes=64, name="grouped1")
+        operand1[0] = new_operand("1")
+        for g in range(PASSES):
+            sixfold[0, g] = new_bank()
+            base_term(0, g, sixfold[0, g], 0)
+            first_state_half(0, pairs1[0], g)
+            regroup_half(turn_half(pairs1[0], g), grouped1[0], g)
+        for h in range(HALVES):
+            base_term(0, h, sixfold[0, h], 1)
+        dv(1)
+        s1(1)
+        t1(1)
+        doubled_k3[0] = new_banks()
+        for g in range(PASSES):
+            quantise_half(grouped1[0], operand1[0], g)
+            multiply_half(doubled_k3[0], operand1[0], g, g == 0, g == PASSES - 1)
+        dv(2)
+        merge(-1, 0, MERGES)
+        merge(-1, 1, MERGES)
+        q1(1)
+        k3(1)
+        for i in range(B - 1):
+            run(ORDERS[i], i)
+        for g in range(PASSES):
+            q2(7, g)
+            k4(7, g)
+        load_last_out()
+        fin(6)
+        store_last_out()
+        fin(7)

@@ -29,7 +29,7 @@ ON_TENSOR = (0, 2, 3, 4)
 TENSOR_ROUND = {0: ((2, 0),), 1: ((2, 1),), 2: ((3, 0),), 3: ((3, 1),), 4: ((4, 0),), 5: ((4, 1),)}
 DOUBLED_ON_SCALAR = (5, 6, 7)
 LEAD = 3
-ORDERS = {0: "s2 t2 s1a t1 base0 dv3 dbl m q2 k4 base ev", 1: "s2 dv4 t2 s1b t1 base ev s1 dy q1 k3 dbl m q2 g k4 fin", 2: "s2 base ev t2 t1 s1 sx dy q1 k3 dbl add m q2 g k4 fin", 3: "s2 base ev t2 t1 s1 sx dy q1 k3 dbl add m q2 g k4 fin", 4: "s2 base ev t2 t1 s1 sx dy q1 k3 dbl add m q2 g k4 fin", 5: "s2 base ev t2 t1 s1 sx dy q1 k3 dbl add m q2 q7 g k4 fin k7", 6: "s2 t2 fin sx dbl s7a t7a s7b t7b q2 k4 add7"}
+ORDERS = {0: "s2 t2 s1a t1 base0 dv3 dbl m q2 k4 base ev", 1: "s2 dv4 t2 s1b t1 base ev s1 dy q1 k3 dbl m q2 g k4 fin", 2: "s2 base ev t2 t1 s1 sx dy q1 k3 dbl add m q2 g k4 fin", 3: "s2 base ev t2 t1 s1 sx dy q1 k3 dbl add m q2 g k4 fin", 4: "s2 base ev t2 t1 s1 sx dy q1 k3 dbl add m q2 g k4 fin", 5: "s2 base ev t2 t1 s1 sx dy q1 k3 dbl add m q2 q7 g k4 fin k7", 6: "s2 t2 fin rows sx dbl s7a t7a s7b t7b q2 k4 add7"}
 TERM_ORDER = (0, 2, 1)
 MERGES = {-1: ("k2 and y", 1), 0: ("k1", 1), 1: ("k2 and y", 5), 2: ("k2 and y", 6), 3: ("k2 and y", 7), 4: ("k1", 6), 5: ("k1", 7)}
 GPSIMD_ROUND = {2: ("next", 1), 3: ("next", 5), 4: ("k1", 5), 5: ("next", 6), 6: ("next", 7)}
@@ -128,12 +128,12 @@ def tile_sindylossmixin_pa_kernel(
 
         def load_last_out():
             for start, stop, step in LAST_ROWS:
-                nc.sync.dma_start(out=last_out[:, spots(start, stop, step), :], in_=spread(out[start:stop:step, P - 1, :]))
+                nc.scalar.dma_start(out=last_out[:, spots(start, stop, step), :], in_=spread(out[start:stop:step, P - 1, :]))
 
         def store_last_out():
             nc.gpsimd.tensor_tensor(out=last_fixed[:], in0=last_out[:], in1=last_next[:], op=SUBTRACT)
             for start, stop, step in LAST_ROWS:
-                nc.sync.dma_start(out=spread(out[start:stop:step, P - 1, :]), in_=last_fixed[:, spots(start, stop, step), :])
+                nc.scalar.dma_start(out=spread(out[start:stop:step, P - 1, :]), in_=last_fixed[:, spots(start, stop, step), :])
 
         def spread(rows):
             return rows.rearrange("b (p c) -> p b c", p=ROW_PARTS)
@@ -501,6 +501,8 @@ def tile_sindylossmixin_pa_kernel(
                     q1(7)
                 elif step == "k7":
                     k3(7)
+                elif step == "rows":
+                    load_last_out()
                 elif step == "add7":
                     add_k3(7)
                 elif step == "s7a":
@@ -552,7 +554,6 @@ def tile_sindylossmixin_pa_kernel(
         for g in range(PASSES):
             q2(7, g)
             k4(7, g)
-        load_last_out()
-        fin(6)
         store_last_out()
+        fin(6)
         fin(7)

@@ -29,7 +29,7 @@ ON_TENSOR = (0, 2, 3, 4)
 TENSOR_ROUND = {0: ((2, 0),), 1: ((2, 1),), 2: ((3, 0),), 3: ((3, 1),), 4: ((4, 0),), 5: ((4, 1),)}
 DOUBLED_ON_SCALAR = (5, 6, 7)
 LEAD = 3
-ORDERS = {0: "s2 t2 s1a t1 base0 dv3 dbl m q2 k4 base ev", 1: "s2 dv4 t2 s1b t1 base ev s1 dy q1 k3 dbl m q2 g k4 fin", 2: "s2 base ev t2 t1 s1 sx dy q1 k3 dbl add m q2 g k4 fin", 3: "s2 base ev t2 t1 s1 sx dy q1 k3 dbl add m q2 g k4 fin", 4: "s2 base ev t2 t1 s1 sx dy q1 k3 dbl add m q2 g k4 fin", 5: "s2 base ev t2 t1 s1 sx dy q1 k3 dbl add m q2 q7 g k4 fin k7", 6: "s2 t2 fin rows sx dbl s7a t7a s7b t7b q2 k4 add7"}
+ORDERS = {0: "s2 dv2 t2 s1a t1 base0 dbl m q2 dv3 k4 base ev", 1: "s2 dv4 t2 s1b t1 base ev s1 dy q1 k3 dbl m q2 g k4 fin", 2: "s2 base ev t2 t1 s1 sx dy q1 k3 dbl add m q2 g k4 fin", 3: "s2 base ev t2 t1 s1 sx dy q1 k3 dbl add m q2 g k4 fin", 4: "s2 base ev t2 t1 s1 sx dy q1 k3 dbl add m q2 g k4 fin", 5: "s2 base ev t2 t1 s1 sx dy q1 k3 dbl add m q2 q7 g k4 fin k7", 6: "s2 t2 fin rows sx dbl s7a t7a s7b t7b q2 k4 add7"}
 TERM_ORDER = (0, 2, 1)
 MERGES = {-1: ("k2 and y", 1), 0: ("k1", 1), 1: ("k2 and y", 5), 2: ("k2 and y", 6), 3: ("k2 and y", 7), 4: ("k1", 6), 5: ("k1", 7)}
 GPSIMD_ROUND = {2: ("next", 1), 3: ("next", 5), 4: ("k1", 5), 5: ("next", 6), 6: ("next", 7)}
@@ -332,16 +332,23 @@ def tile_sindylossmixin_pa_kernel(
         load_w_scales()
         load_w_words()
         load_state(2)
-        load_k1(0)
-        load_k1(2)
-        load_state(3)
-        load_next(1)
         load_k1(1)
+        load_k1(0)
+        load_state(3)
+        load_k1(2)
+        load_state(4)
+        load_state(5)
+        load_next(1)
         load_k1(3)
-        for b in range(4, B):
-            load_state(b)
-            load_k1(b)
-            load_next(b)
+        load_next(5)
+        load_k1(5)
+        load_state(6)
+        load_k1(4)
+        load_next(6)
+        load_k1(6)
+        load_state(7)
+        load_next(7)
+        load_k1(7)
         load_last_next()
 
         pairs1, grouped1, grouped2, operand1, operand2 = {}, {}, {}, {}, {}
@@ -491,6 +498,8 @@ def tile_sindylossmixin_pa_kernel(
                     s1(3)
                 elif step == "dv4":
                     dv(4)
+                elif step == "dv2":
+                    dv(2)
                 elif step == "dv3":
                     dv(3)
                 elif step == "base0":
@@ -544,7 +553,6 @@ def tile_sindylossmixin_pa_kernel(
         for g in range(PASSES):
             quantise_half(grouped1[0], operand1[0], g)
             multiply_half(doubled_k3[0], operand1[0], g, g == 0, g == PASSES - 1)
-        dv(2)
         merge(-1, 0, MERGES)
         merge(-1, 1, MERGES)
         q1(1)

@@ -26,17 +26,17 @@ HALVES = H // N_TILE
 FLOPS = 2 * 2 * (B * P) * H * H
 
 ON_TENSOR = (0, 2, 3, 4)
-TENSOR_ROUND = {0: ((2, 0),), 1: ((2, 1),), 2: ((3, 0),), 3: ((3, 1),), 4: ((4, 0),), 5: ((4, 1),)}
+TENSOR_ROUND = {1: ((2, 0),), 2: ((2, 1),), 3: ((3, 0),), 4: ((3, 1), (4, 0)), 5: ((4, 1),)}
 DOUBLED_ON_SCALAR = (5, 6, 7)
 LEAD = 3
-ORDERS = {0: "s2 dv2 t2 s1a t1 base0 dbl m q2 dv3 k4 base ev", 1: "s2 dv4 t2 s1b t1 base ev s1 dy q1 k3 dbl m q2 g k4 fin", 2: "s2 base ev t2 t1 s1 sx dy q1 k3 dbl add m q2 g k4 fin", 3: "s2 base ev t2 t1 s1 sx dy q1 k3 dbl add m q2 g k4 fin", 4: "s2 base ev t2 t1 s1 sx dy q1 k3 dbl add m q2 g k4 fin", 5: "s2 base ev t2 t1 s1 sx dy q1 k3 dbl add m q2 q7 g k4 fin k7", 6: "s2 t2 fin rows sx dbl s7a t7a s7b t7b q2 k4 add7"}
+ORDERS = {0: "ds2 s2 t2 s1a t1 base0 dbl m q2 dv3 k4 base ev", 1: "s2 dv4 t2 s1b t1 base ev s1 dy q1 k3 dbl m q2 add g k4 fin", 2: "s2 base ev t2 t1 s1 sx dy q1 k3 dbl m q2 add g k4 fin", 3: "s2 base ev t2 t1 s1 sx dy q1 k3 dbl m q2 add g k4 fin", 4: "s2 base ev t2 t1 s1 sx dy q1 k3 dbl m q2 add g k4 fin", 5: "s2 base ev t2 t1 s1 sx dy q1 k3 dbl m q2 add q7 g k4 fin k7", 6: "g s2 t2 fin rows sx dbl add s7a t7a s7b t7b rowsb q2 k4 add7"}
 TERM_ORDER = (0, 2, 1)
-MERGES = {-1: ("k2 and y", 1), 0: ("k1", 1), 1: ("k2 and y", 5), 2: ("k2 and y", 6), 3: ("k2 and y", 7), 4: ("k1", 6), 5: ("k1", 7)}
-GPSIMD_ROUND = {2: ("next", 1), 3: ("next", 5), 4: ("k1", 5), 5: ("next", 6), 6: ("next", 7)}
-UNDOUBLED = (7,)
+MERGES = {-1: ("k2 and y", 1), 0: ("k1", 1), 2: ("k2 and y", 5), 3: ("k2 and y", 6), 4: ("k2 and y", 7), 5: ("k1", 7)}
+GPSIMD_ROUND = {2: ("next", 1), 3: ("next", 5), 4: ("k1", 5), 5: ("next", 6), 6: ("k1", 6), 7: ("next", 7)}
+UNDOUBLED = (1, 7)
 MERGES2 = {}
-SIXTH_ROUND = {2: 5}
-LAST_ROWS = ((0, 1, 1), (2, 5, 1))
+SIXTH_ROUND = {2: 5, 4: 6}
+LAST_ROWS = ((0, 1, 1), (2, 4, 1), (4, 5, 1))
 ROW_PARTS = 32
 assert len(ON_TENSOR) * 3 * HALVES * 2 * P * P * N_TILE <= FLOPS // 10
 
@@ -126,14 +126,17 @@ def tile_sindylossmixin_pa_kernel(
             for start, stop, step in LAST_ROWS:
                 nc.sync.dma_start(out=last_next[:, spots(start, stop, step), :], in_=spread(x[start:stop:step, P, :]))
 
-        def load_last_out():
-            for start, stop, step in LAST_ROWS:
+        def load_last_out(ranges):
+            for start, stop, step in ranges:
                 nc.scalar.dma_start(out=last_out[:, spots(start, stop, step), :], in_=spread(out[start:stop:step, P - 1, :]))
 
-        def store_last_out():
-            nc.gpsimd.tensor_tensor(out=last_fixed[:], in0=last_out[:], in1=last_next[:], op=SUBTRACT)
-            for start, stop, step in LAST_ROWS:
-                nc.scalar.dma_start(out=spread(out[start:stop:step, P - 1, :]), in_=last_fixed[:, spots(start, stop, step), :])
+        def store_last_out(ranges):
+            for start, stop, step in ranges:
+                cols = spots(start, stop, step)
+                nc.gpsimd.tensor_tensor(
+                    out=last_fixed[:, cols, :], in0=last_out[:, cols, :], in1=last_next[:, cols, :], op=SUBTRACT
+                )
+                nc.scalar.dma_start(out=spread(out[start:stop:step, P - 1, :]), in_=last_fixed[:, cols, :])
 
         def spread(rows):
             return rows.rearrange("b (p c) -> p b c", p=ROW_PARTS)
@@ -500,6 +503,12 @@ def tile_sindylossmixin_pa_kernel(
                     dv(4)
                 elif step == "dv2":
                     dv(2)
+                elif step == "ds2":
+                    doubled_y[2] = double_y(2)
+                elif step == "ds3":
+                    doubled_y[3] = double_y(3)
+                elif step == "ds4":
+                    doubled_y[4] = double_y(4)
                 elif step == "dv3":
                     dv(3)
                 elif step == "base0":
@@ -511,7 +520,10 @@ def tile_sindylossmixin_pa_kernel(
                 elif step == "k7":
                     k3(7)
                 elif step == "rows":
-                    load_last_out()
+                    load_last_out(LAST_ROWS[:2])
+                elif step == "rowsb":
+                    load_last_out(LAST_ROWS[2:])
+                    store_last_out(LAST_ROWS)
                 elif step == "add7":
                     add_k3(7)
                 elif step == "s7a":
@@ -562,6 +574,5 @@ def tile_sindylossmixin_pa_kernel(
         for g in range(PASSES):
             q2(7, g)
             k4(7, g)
-        store_last_out()
         fin(6)
         fin(7)

@@ -26,10 +26,10 @@ HALVES = H // N_TILE
 FLOPS = 2 * 2 * (B * P) * H * H
 
 ON_TENSOR = (0, 2, 3, 4)
-TENSOR_ROUND = {1: ((2, 0),), 2: ((2, 1),), 3: ((3, 0),), 4: ((3, 1), (4, 0)), 5: ((4, 1),)}
+TENSOR_ROUND = {1: ((2, 0), (2, 1)), 2: ((3, 0),), 3: ((3, 1),), 4: ((4, 0),), 5: ((4, 1),)}
 DOUBLED_ON_SCALAR = (5, 6, 7)
 LEAD = 3
-ORDERS = {0: "ds2 s2 t2 s1a t1 base0 dbl m q2 dv3 k4 base ev", 1: "s2 dv4 t2 s1b t1 base ev s1 dy q1 k3 dbl m q2 add g k4 fin", 2: "s2 base ev t2 t1 s1 sx dy q1 k3 dbl m q2 add g k4 fin", 3: "s2 base ev t2 t1 s1 sx dy q1 k3 dbl m q2 add g k4 fin", 4: "s2 base ev t2 t1 s1 sx dy q1 k3 dbl m q2 add g k4 fin", 5: "s2 base ev t2 t1 s1 sx dy q1 k3 dbl m q2 add q7 g k4 fin k7", 6: "g s2 t2 fin rows sx dbl add s7a t7a s7b t7b rowsb q2 k4 add7"}
+ORDERS = {0: "ds2 s2 t2 s1a t1 ds3 base0 dbl m q2 k4 base ev", 1: "s2 dv4 t2 s1b t1 base ev q1 k3 s1 dy dbl m q2 add g k4 fin", 2: "s2 t2 t1 base ev q1 k3 s1 sx dy dbl m q2 add g k4 fin", 3: "s2 t2 t1 base ev q1 k3 s1 sx dy dbl m q2 add g k4 fin", 4: "s2 t2 t1 base ev q1 k3 s1 sx dy dbl m q2 add g k4 fin", 5: "s2 t2 t1 base ev q1 k3 s1 sx dy dbl m q2 add q7 g k4 fin k7", 6: "g s2 t2 fin rows sx dbl add s7a t7a s7b t7b rowsb q2 k4 add7"}
 TERM_ORDER = (0, 2, 1)
 MERGES = {-1: ("k2 and y", 1), 0: ("k1", 1), 2: ("k2 and y", 5), 3: ("k2 and y", 6), 4: ("k2 and y", 7), 5: ("k1", 7)}
 GPSIMD_ROUND = {2: ("next", 1), 3: ("next", 5), 4: ("k1", 5), 5: ("next", 6), 6: ("k1", 6), 7: ("next", 7)}

from contextlib import ExitStack

import concourse.masks as masks
import concourse.mybir as mybir

F32 = mybir.dt.float32
BF16 = mybir.dt.bfloat16
I32 = mybir.dt.int32
U32 = mybir.dt.uint32
U8 = mybir.dt.uint8
FP8X4 = mybir.dt.float8_e4m3fn_x4
FP4X4 = mybir.dt.float4_e2m1fn_x4
MULT = mybir.AluOpType.mult
ADD = mybir.AluOpType.add
SUBTRACT = mybir.AluOpType.subtract
COPY = mybir.ActivationFunctionType.Copy

P = 128
B = 8
H = 1024
K_PASS = 512
PASSES = H // K_PASS
N_TILE = 512
HALVES = H // N_TILE

FLOPS = 2 * 2 * (B * P) * H * H

ON_TENSOR = (0, 2, 3, 4)
TENSOR_ROUND = {1: ((2, 0), (2, 1)), 2: ((3, 0),), 3: ((3, 1),), 4: ((4, 0),), 5: ((4, 1),)}
DOUBLED_ON_SCALAR = (5, 6, 7)
LEAD = 3
ORDERS = {0: "ds2 s2 t2 s1a t1 ds3 base0 dbl m q2 k4 base ev", 1: "s2 dv4 t2 s1b t1 base ev q1 k3 s1 dy dbl m q2 add g k4 fin", 2: "s2 t2 t1 base ev q1 k3 s1 sx dy dbl m q2 add g k4 fin", 3: "s2 t2 t1 base ev q1 k3 s1 sx dy dbl m q2 add g k4 fin", 4: "s2 t2 t1 base ev q1 k3 s1 sx dy dbl m q2 add g k4 fin", 5: "s2 t2 t1 base ev q1 k3 s1 sx dy dbl m q2 add q7 g k4 fin k7", 6: "g s2 t2 fin rows sx dbl add s7a t7a s7b t7b rowsb q2 k4 add7"}
TERM_ORDER = (0, 2, 1)
MERGES = {-1: ("k2 and y", 1), 0: ("k1", 1), 2: ("k2 and y", 5), 3: ("k2 and y", 6), 4: ("k2 and y", 7), 5: ("k1", 7)}
GPSIMD_ROUND = {2: ("next", 1), 3: ("next", 5), 4: ("k1", 5), 5: ("next", 6), 6: ("k1", 6), 7: ("next", 7)}
UNDOUBLED = (1, 7)
MERGES2 = {}
SIXTH_ROUND = {2: 5, 4: 6}
LAST_ROWS = ((0, 1, 1), (2, 4, 1), (4, 5, 1))
ROW_PARTS = 32
assert len(ON_TENSOR) * 3 * HALVES * 2 * P * P * N_TILE <= FLOPS // 10


def tile_sindylossmixin_pa_kernel(
    tc, x, k1, k2, coefficients_words, coefficients_scales, out
):
    nc = tc.nc
    with ExitStack() as ctx:
        ctx.enter_context(tc.manual_schedule())
        const = ctx.enter_context(tc.tile_pool(name="const", bufs=1))
        inputs = ctx.enter_context(tc.tile_pool(name="inputs", bufs=1))
        sums = ctx.enter_context(tc.tile_pool(name="sums", bufs=B))
        operands = ctx.enter_context(tc.tile_pool(name="operands", bufs=4))
        psum_turned = ctx.enter_context(tc.psum_pool(name="psum_turned", bufs=2))
        psum_banks = ctx.enter_context(tc.psum_pool(name="psum_banks", bufs=6))

        identity = const.tile([P, P], F32)
        masks.make_identity(nc, identity[:])
        six_eye = const.tile([P, P], F32)
        difference = const.tile([P, P], BF16)
        one_eye = const.tile([P, P], BF16)
        two_eye = const.tile([P, P], BF16)

        w_words = const.tile([P, PASSES, 2 * H], U8, align_bytes=64)
        w_scales = const.tile([P, PASSES, H], U8, align_bytes=64)
        w_scale_words = w_scales[:].bitcast(I32)
        nc.vector.memset(w_scale_words, 0)
        nc.vector.tensor_scalar_mul(out=six_eye[:], in0=identity[:], scalar1=6.0)
        nc.vector.tensor_scalar_mul(out=one_eye[:], in0=identity[:], scalar1=1.0)
        nc.vector.tensor_scalar_mul(out=two_eye[:], in0=identity[:], scalar1=2.0)
        nc.vector.tensor_tensor(
            out=difference[:, 0 : P - 1], in0=six_eye[:, 0 : P - 1], in1=six_eye[:, 1:P], op=SUBTRACT
        )
        nc.vector.tensor_copy(out=difference[:, P - 1 : P], in_=six_eye[:, P - 1 : P])

        y_all = inputs.tile([P, B, H], BF16)
        next_all = inputs.tile([P, B, H], BF16)
        k1_all = inputs.tile([P, B, H], BF16)
        k2_all = inputs.tile([P, B, H], BF16)
        row_words = H // ROW_PARTS
        last_next = inputs.tile([ROW_PARTS, len(ON_TENSOR), row_words], BF16)
        last_out = inputs.tile([ROW_PARTS, len(ON_TENSOR), row_words], F32)
        sync_f32 = inputs.tile([P, B], F32)
        sync_u32 = inputs.tile([P, B], U32)
        last_fixed = inputs.tile([ROW_PARTS, len(ON_TENSOR), row_words], F32)

        def exists(b):
            return 0 <= b < B

        def half(h):
            return slice(h * N_TILE, (h + 1) * N_TILE)

        def load_w_scales():
            for r in range(4):
                nc.sync.dma_start(
                    out=w_scale_words[r:P:32, :, :],
                    in_=coefficients_scales[:, r:16:4, :].bitcast(I32).rearrange("g q c -> q g c"),
                )

        def load_w_words():
            for g in range(PASSES):
                nc.sync.dma_start(
                    out=w_words[:, g, :].bitcast(I32), in_=coefficients_words[g].bitcast(I32)
                )

        def load_state_half(b, g):
            nc.sync.dma_start(out=y_all[:, b, half(g)], in_=x[b, 0:P, half(g)])
            nc.sync.dma_start(out=k2_all[:, b, half(g)], in_=k2[b * P : (b + 1) * P, half(g)])

        def load_state(b):
            nc.sync.dma_start(out=y_all[:, b, :], in_=x[b, 0:P, :])
            nc.sync.dma_start(out=k2_all[:, b, :], in_=k2[b * P : (b + 1) * P, :])

        def load_k1(b):
            nc.sync.dma_start(out=k1_all[:, b, :], in_=k1[b * P : (b + 1) * P, :])

        def load_next(b):
            if b not in ON_TENSOR:
                nc.sync.dma_start(out=next_all[:, b, :], in_=x[b, 1 : P + 1, :])

        def spots(start, stop, step):
            first = ON_TENSOR.index(start)
            return slice(first, first + len(range(start, stop, step)))

        def load_last_next():
            for start, stop, step in LAST_ROWS:
                nc.sync.dma_start(out=last_next[:, spots(start, stop, step), :], in_=spread(x[start:stop:step, P, :]))

        def load_last_out(ranges):
            for start, stop, step in ranges:
                nc.scalar.dma_start(out=last_out[:, spots(start, stop, step), :], in_=spread(out[start:stop:step, P - 1, :]))

        def store_last_out(ranges):
            for start, stop, step in ranges:
                cols = spots(start, stop, step)
                nc.gpsimd.tensor_tensor(
                    out=last_fixed[:, cols, :], in0=last_out[:, cols, :], in1=last_next[:, cols, :], op=SUBTRACT
                )
                nc.scalar.dma_start(out=spread(out[start:stop:step, P - 1, :]), in_=last_fixed[:, cols, :])

        def spread(rows):
            return rows.rearrange("b (p c) -> p b c", p=ROW_PARTS)

        def first_state(b):
            pairs = operands.tile([P, H], BF16, name="pairs1")
            twice = doubled_y[b]
            nc.vector.tensor_tensor(
                out=pairs[:].rearrange("m (u q e) -> m u q e", u=2, e=2),
                in0=twice[:].rearrange("m (q u e) -> m u q e", u=2, e=2),
                in1=k2_all[:, b, :].rearrange("m (q u e) -> m u q e", u=2, e=2),
                op=ADD,
            )
            return pairs

        def first_state_half(b, pairs, g):
            for u in range(2):
                first = u * K_PASS + g * 2 * P
                nc.vector.scalar_tensor_tensor(
                    out=pairs[:, first : first + 2 * P].rearrange("m (o p e) -> m o p e", o=1, e=2),
                    in0=y_all[:, b, half(g)].rearrange("m (p u e) -> m u p e", u=2, e=2)[:, u : u + 1],
                    scalar=2.0,
                    in1=k2_all[:, b, half(g)].rearrange("m (p u e) -> m u p e", u=2, e=2)[:, u : u + 1],
                    op0=MULT,
                    op1=ADD,
                )

        def double_on_vector(b):
            twice = operands.tile([P, H], BF16, name="twice")
            nc.vector.tensor_scalar_mul(out=twice[:], in0=y_all[:, b, :], scalar1=2.0)
            return twice

        def double_y(b):
            twice = operands.tile([P, H], BF16, name="twice")
            nc.scalar.activation(out=twice[:], in_=y_all[:, b, :], func=COPY, scale=2.0)
            return twice

        def second_state(b, doubled_k3):
            pairs = operands.tile([P, H], BF16, name="pairs2")
            for g in range(PASSES):
                second_state_half(b, doubled_k3, pairs, g)
            return pairs

        def second_state_half(b, doubled_k3, pairs, g):
            for u in range(2):
                first = u * K_PASS + g * 2 * P
                nc.vector.scalar_tensor_tensor(
                    out=pairs[:, first : first + 2 * P].rearrange("m (o p e) -> m o p e", o=1, e=2),
                    in0=doubled_k3[g].rearrange("m (p u e) -> m u p e", u=2, e=2)[:, u : u + 1],
                    scalar=0.5,
                    in1=y_all[:, b, half(g)].rearrange("m (p u e) -> m u p e", u=2, e=2)[:, u : u + 1],
                    op0=MULT,
                    op1=ADD,
                )

        def turn_half(pairs, g):
            words = pairs[:].bitcast(F32)
            turned = psum_turned.tile([P, 2 * PASSES, P], F32, name="turned")
            for u in range(2):
                first = (u * PASSES + g) * P
                nc.tensor.transpose(turned[:, u, :], words[:, first : first + P], identity[:])
            return turned

        def regroup_half(turned, grouped, g):
            nc.scalar.copy(
                out=grouped[:, g * K_PASS : (g + 1) * K_PASS].bitcast(F32).rearrange("p (m u) -> p m u", u=2),
                in_=turned[:, 0:2, :].rearrange("p u m -> p m u"),
            )

        def quantise_half(grouped, operand, g):
            codes, scales = operand
            nc.vector.quantize_mx(
                out=codes[:, g * P : (g + 1) * P].bitcast(FP8X4),
                scales=scales[:, g * P : (g + 1) * P],
                in_=grouped[:, g * K_PASS : (g + 1) * K_PASS],
            )

        def multiply_half(banks, operand, g, opens, closes):
            codes, scales = operand
            rows = slice(g * P, (g + 1) * P)
            for h in range(HALVES):
                nc.tensor.matmul_mx(
                    out=banks[h],
                    lhsT=codes[:, rows].bitcast(FP8X4),
                    lhsT_scale=scales[:, rows],
                    rhs=w_words[:, g, 2 * h * N_TILE : 2 * (h + 1) * N_TILE].bitcast(FP4X4),
                    rhs_scale=w_scales[:, g, half(h)],
                    start=opens,
                    stop=closes,
                )

        def turn(pairs):
            words = pairs[:].bitcast(F32)
            turned = psum_turned.tile([P, 2 * PASSES, P], F32, name="turned")
            for g in range(PASSES):
                for u in range(2):
                    first = (u * PASSES + g) * P
                    nc.tensor.transpose(turned[:, 2 * g + u, :], words[:, first : first + P], identity[:])
            return turned

        def regroup(turned, name):
            grouped = operands.tile([P, H], BF16, align_bytes=64, name=name)
            nc.scalar.copy(
                out=grouped[:].bitcast(F32).rearrange("p (g m u) -> p g m u", g=PASSES, u=2),
                in_=turned[:].rearrange("p (g u) m -> p g m u", u=2),
            )
            return grouped

        def new_operand(name):
            codes = operands.tile([P, PASSES * P], U32, align_bytes=64, name="codes" + name)
            scales = operands.tile([P, PASSES * P], U8, align_bytes=64, name="scales" + name)
            return codes, scales

        def quantise(grouped, name):
            codes, scales = new_operand(name)
            nc.vector.quantize_mx(out=codes[:].bitcast(FP8X4), scales=scales[:], in_=grouped[:])
            return codes, scales

        def new_banks():
            banks = []
            for h in range(HALVES):
                bank = psum_banks.tile([P, N_TILE], F32, name="bank")
                banks.append(bank[:])
            return banks

        def multiply(banks, operand, opens, closes):
            codes, scales = operand
            for h in range(HALVES):
                for g in range(PASSES):
                    rows = slice(g * P, (g + 1) * P)
                    nc.tensor.matmul_mx(
                        out=banks[h],
                        lhsT=codes[:, rows].bitcast(FP8X4),
                        lhsT_scale=scales[:, rows],
                        rhs=w_words[:, g, 2 * h * N_TILE : 2 * (h + 1) * N_TILE].bitcast(FP4X4),
                        rhs_scale=w_scales[:, g, half(h)],
                        start=(opens and g == 0),
                        stop=(closes and g == PASSES - 1),
                    )

        def add_scaled(total, term, factor):
            nc.vector.scalar_tensor_tensor(
                out=total, in0=term, scalar=factor, in1=total, op0=MULT, op1=ADD
            )

        def base_term(b, h, bank, n):
            eye, source = ((difference, y_all), (one_eye, k1_all), (two_eye, k2_all))[TERM_ORDER[n]]
            nc.tensor.matmul(out=bank, lhsT=eye[:], rhs=source[:, b, half(h)], start=(n == 0), stop=(n == 2))

        def new_bank():
            bank = psum_banks.tile([P, N_TILE], F32, name="bank")
            return bank[:]

        def base_on_tensor(b, h):
            bank = new_bank()
            for n in range(3):
                base_term(b, h, bank, n)
            return bank

        def base_out_of_psum(base, bank, h):
            nc.scalar.activation(out=base[:, half(h)], in_=bank, func=COPY, scale=1.0 / 6.0)

        def minus_next(b):
            nc.gpsimd.tensor_tensor(out=total[b][:], in0=total[b][:], in1=next_all[:, b, :], op=SUBTRACT)

        def merge(i, h, table):
            what, b = table.get(i, ("", 0))
            if what == "k2 and y":
                if h == 0:
                    total[b] = sums.tile([P, H], F32, name="total")
                nc.vector.scalar_tensor_tensor(
                    out=total[b][:, half(h)], in0=k2_all[:, b, half(h)], scalar=1.0 / 3.0,
                    in1=y_all[:, b, half(h)], op0=MULT, op1=ADD,
                )
            elif what == "k1":
                add_scaled(total[b][:, half(h)], k1_all[:, b, half(h)], 1.0 / 6.0)

        def merge_on_gpsimd(i):
            what, b = GPSIMD_ROUND.get(i, ("", 0))
            if what == "next":
                minus_next(b)
            elif what == "k1":
                if i - 1 in MERGES:
                    nc.gpsimd.tensor_copy(out=sync_f32[:, i : i + 1], in_=total[MERGES[i - 1][1]][:, H - 1 : H])
                elif i in operand1:
                    nc.gpsimd.tensor_copy(out=sync_u32[:, i : i + 1], in_=operand1[i][0][:, 0:1])
                nc.gpsimd.tensor_tensor(out=total[b][:], in0=total[b][:], in1=sixth[b][:], op=ADD)

        def sixth_of_k1(b):
            sixth[b] = operands.tile([P, H], F32, name="sixth")
            nc.scalar.activation(out=sixth[b][:], in_=k1_all[:, b, :], func=COPY, scale=1.0 / 6.0)

        for g in range(PASSES):
            load_state_half(0, g)
        load_state(1)
        load_w_scales()
        load_w_words()
        load_state(2)
        load_k1(1)
        load_k1(0)
        load_state(3)
        load_k1(2)
        load_state(4)
        load_state(5)
        load_next(1)
        load_k1(3)
        load_next(5)
        load_k1(5)
        load_state(6)
        load_k1(4)
        load_next(6)
        load_k1(6)
        load_state(7)
        load_next(7)
        load_k1(7)
        load_last_next()

        pairs1, grouped1, grouped2, operand1, operand2 = {}, {}, {}, {}, {}
        doubled_k3, last, total, sixfold, doubled_y = {}, {}, {}, {}, {}
        sixth = {}

        def finish(b, h):
            add_scaled(total[b][:, half(h)], last[b][h], 1.0 / 6.0)
            nc.sync.dma_start(out=out[b, :, half(h)], in_=total[b][:, half(h)])

        def evacuate(b, h):
            if h == 0:
                total[b] = sums.tile([P, H], F32, name="total")
            base_out_of_psum(total[b], sixfold[b, h], h)

        def start_next(b):
            operand1[b] = quantise(grouped1[b], "1")
            doubled_k3[b] = new_banks()
            multiply(doubled_k3[b], operand1[b], True, True)

        def double(b):
            if b not in UNDOUBLED:
                last[b] = new_banks()
                multiply(last[b], operand1[b], True, False)

        def add_k3(b):
            if b in UNDOUBLED:
                for h in range(HALVES):
                    add_scaled(total[b][:, half(h)], doubled_k3[b][h], 1.0 / 6.0)

        pairs2 = {}

        def s2(i, g=None):
            if g is None:
                pairs2[i] = second_state(i, doubled_k3[i])
            else:
                if g == 0:
                    pairs2[i] = operands.tile([P, H], BF16, name="pairs2")
                second_state_half(i, doubled_k3[i], pairs2[i], g)

        def t2(i, g=None):
            if g is None:
                grouped2[i] = regroup(turn(pairs2[i]), "grouped2")
            else:
                if g == 0:
                    grouped2[i] = operands.tile([P, H], BF16, align_bytes=64, name="grouped2")
                regroup_half(turn_half(pairs2[i], g), grouped2[i], g)

        def t1(b):
            if exists(b):
                grouped1[b] = regroup(turn(pairs1[b]), "grouped1")

        def q1(b):
            operand1[b] = quantise(grouped1[b], "1")

        def k3(b):
            doubled_k3[b] = new_banks()
            multiply(doubled_k3[b], operand1[b], True, True)

        def q2(i, g=None):
            if g is None:
                operand2[i] = quantise(grouped2[i], "2")
            else:
                if g == 0:
                    operand2[i] = new_operand("2")
                quantise_half(grouped2[i], operand2[i], g)

        def k4(i, g=None):
            if i in UNDOUBLED and not g:
                last[i] = new_banks()
            if g is None:
                multiply(last[i], operand2[i], i in UNDOUBLED, True)
            else:
                multiply_half(last[i], operand2[i], g, i in UNDOUBLED and g == 0, g == PASSES - 1)

        def s1(b):
            if exists(b):
                pairs1[b] = first_state(b)

        def fin(b, h=None):
            if exists(b):
                for n in range(HALVES) if h is None else (h,):
                    finish(b, n)

        def base(i):
            for b, h in TENSOR_ROUND.get(i, ()):
                sixfold[b, h] = base_on_tensor(b, h)

        def ev(i):
            for b, h in TENSOR_ROUND.get(i, ()):
                evacuate(b, h)

        def sx(i):
            if i in SIXTH_ROUND:
                sixth_of_k1(SIXTH_ROUND[i])

        def dy(b):
            if b in DOUBLED_ON_SCALAR:
                doubled_y[b] = double_y(b)

        def dv(b):
            doubled_y[b] = double_on_vector(b)

        def run(order, i):
            for step in order.split():
                if step == "q1":
                    q1(i + 1)
                elif step == "k3":
                    k3(i + 1)
                elif step == "s2":
                    s2(i)
                elif step == "t2":
                    t2(i)
                elif step == "t1":
                    t1(i + 2)
                elif step == "fin":
                    fin(i - 1)
                elif step == "dbl":
                    double(i)
                elif step == "base":
                    base(i)
                elif step == "ev":
                    ev(i)
                elif step == "s1":
                    s1(i + LEAD)
                elif step == "add":
                    add_k3(i)
                elif step == "ma":
                    merge(i, 0, MERGES)
                elif step == "mb":
                    merge(i, 1, MERGES)
                elif step == "na":
                    merge(i, 0, MERGES2)
                elif step == "nb":
                    merge(i, 1, MERGES2)
                elif step == "q2":
                    q2(i)
                elif step == "k4":
                    k4(i)
                elif step == "sx":
                    sx(i)
                elif step == "dy":
                    dy(i + LEAD + 1)
                elif step == "s1a":
                    s1(2)
                elif step == "s1b":
                    s1(3)
                elif step == "dv4":
                    dv(4)
                elif step == "dv2":
                    dv(2)
                elif step == "ds2":
                    doubled_y[2] = double_y(2)
                elif step == "ds3":
                    doubled_y[3] = double_y(3)
                elif step == "ds4":
                    doubled_y[4] = double_y(4)
                elif step == "dv3":
                    dv(3)
                elif step == "base0":
                    for h in range(HALVES):
                        base_term(0, h, sixfold[0, h], 2)
                        evacuate(0, h)
                elif step == "q7":
                    q1(7)
                elif step == "k7":
                    k3(7)
                elif step == "rows":
                    load_last_out(LAST_ROWS[:2])
                elif step == "rowsb":
                    load_last_out(LAST_ROWS[2:])
                    store_last_out(LAST_ROWS)
                elif step == "add7":
                    add_k3(7)
                elif step == "s7a":
                    s2(7, 0)
                elif step == "t7a":
                    t2(7, 0)
                elif step == "s7b":
                    s2(7, 1)
                elif step == "t7b":
                    t2(7, 1)
                elif step == "f6":
                    fin(6)
                elif step == "s7":
                    for g in range(PASSES):
                        s2(7, g)
                        t2(7, g)
                elif step == "dbl7":
                    double(7)
                elif step == "g":
                    merge_on_gpsimd(i + 1)
                elif step == "m":
                    merge(i, 0, MERGES)
                    merge(i, 1, MERGES)

        pairs1[0] = operands.tile([P, H], BF16, name="pairs1")
        grouped1[0] = operands.tile([P, H], BF16, align_bytes=64, name="grouped1")
        operand1[0] = new_operand("1")
        for g in range(PASSES):
            sixfold[0, g] = new_bank()
            base_term(0, g, sixfold[0, g], 0)
            first_state_half(0, pairs1[0], g)
            regroup_half(turn_half(pairs1[0], g), grouped1[0], g)
        for h in range(HALVES):
            base_term(0, h, sixfold[0, h], 1)
        dv(1)
        s1(1)
        t1(1)
        doubled_k3[0] = new_banks()
        for g in range(PASSES):
            quantise_half(grouped1[0], operand1[0], g)
            multiply_half(doubled_k3[0], operand1[0], g, g == 0, g == PASSES - 1)
        merge(-1, 0, MERGES)
        merge(-1, 1, MERGES)
        q1(1)
        k3(1)
        for i in range(B - 1):
            run(ORDERS[i], i)
        for g in range(PASSES):
            q2(7, g)
            k4(7, g)
        fin(6)
        fin(7)
